import numpy as np
import ml_dtypes


def mxq(x, axis, fmt="e4m3"):
    dtype, down = {"e4m3": (ml_dtypes.float8_e4m3fn, 7), "e5m2": (ml_dtypes.float8_e5m2, 14)}[fmt]
    v = np.moveaxis(np.asarray(x, np.float32).astype(ml_dtypes.bfloat16).astype(np.float64), axis, -1)
    blocks = v.reshape(v.shape[:-1] + (-1, 32))
    amax = np.abs(blocks).max(-1, keepdims=True)
    byte = np.maximum(np.where(amax > 0, np.frexp(amax)[1] - 1 + 127, 0) - down, 1)
    scale = np.exp2(byte - 127.0)
    codes = (blocks / scale).astype(np.float32).astype(dtype).astype(np.float64)
    return np.moveaxis((codes * scale).reshape(v.shape), -1, axis)


WIDE = False


def mx_kscale(k):
    if not WIDE:
        return np.ones(k)
    levels = np.array([10, -10, 5, -5, 0])
    if k % 512:
        return np.exp2(np.random.permutation(np.resize(levels, k // 32))).repeat(32)
    a = np.empty((k // 512, 16))
    for p in range(k // 512):
        a[p, :8] = np.random.permutation(np.resize(levels, 8))
        for g in range(8):
            far = levels[np.abs(levels - a[p, g]) >= 10]
            a[p, g + 8] = far[np.random.randint(len(far))]
    return np.exp2(a.ravel()).repeat(32)


BF16 = ml_dtypes.bfloat16


def bf(x):
    return np.asarray(x, np.float32).astype(BF16)


def f64(x):
    return np.asarray(x).astype(np.float64)


B, N, D, C, H, NS = 2, 512, 512, 256, 16, 10
HD = C // H
D4 = (0.4829629131445341, 0.8365163037378079, 0.2241438680420134, -0.1294095225512604)


def causal_multiscale(x_c, scale_gain):
    g = np.exp(scale_gain - scale_gain.max(0, keepdims=True))
    gains = g / g.sum(0, keepdims=True)
    gains_exp = np.repeat(gains, HD, axis=1)
    out = np.zeros_like(x_c)
    for j in range(NS):
        d = 2 ** j
        xp = np.pad(x_c, ((0, 0), (0, 0), (3 * d, 0)))
        y = (D4[0] * xp[:, :, 0 * d:0 * d + N]
             + D4[1] * xp[:, :, 1 * d:1 * d + N]
             + D4[2] * xp[:, :, 2 * d:2 * d + N]
             + D4[3] * xp[:, :, 3 * d:3 * d + N])
        out = out + gains_exp[j][None, :, None] * y
    return out


def setup_inputs():
    s = mx_kscale(D)
    return {"x": bf(np.random.standard_normal((B, N, D)) * s),
            "k_w": bf(np.random.standard_normal((C, D)) / np.sqrt(D) / s[None, :]),
            "k_b": bf(np.random.standard_normal(C) * 0.2),
            "v_w": bf(np.random.standard_normal((C, D)) / np.sqrt(D) / s[None, :]),
            "v_b": bf(np.random.standard_normal(C) * 0.2),
            "scale_gain": bf(np.random.standard_normal((NS, H)) * 0.5)}


def reference(x, k_w, k_b, v_w, v_b, scale_gain):
    xq = mxq(f64(x), 2, "e4m3")
    k = ((xq @ mxq(f64(k_w), 1, "e4m3").T) + f64(k_b)).reshape(B, N, H, HD)
    v = ((xq @ mxq(f64(v_w), 1, "e4m3").T) + f64(v_b)).reshape(B, N, H, HD)
    k_mag = np.sqrt((k * k).sum(-1, keepdims=True))
    field = v * k_mag
    x_c = field.transpose(0, 2, 3, 1).reshape(B, C, N)
    return causal_multiscale(x_c, f64(scale_gain))

@@ -1,0 +1,358 @@
+from contextlib import ExitStack
+
+import concourse.mybir as mybir
+from concourse.masks import make_identity
+
+F32 = mybir.dt.float32
+BF16 = mybir.dt.bfloat16
+U32 = mybir.dt.uint32
+U8 = mybir.dt.uint8
+FP8X4 = mybir.dt.float8_e4m3fn_x4
+ALU = mybir.AluOpType
+ACT = mybir.ActivationFunctionType
+AXIS = mybir.AxisListType
+
+P = 128
+BATCH, TOKENS, WIDTH, CHANNELS, HEADS, SCALES = 2, 512, 512, 256, 16, 10
+HEAD_DIM = CHANNELS // HEADS
+HALVES = CHANNELS // P
+HEADS_PER_HALF = P // HEAD_DIM
+TOKEN_BLOCKS = TOKENS // P
+TAPS = (0.4829629131445341, 0.8365163037378079, 0.2241438680420134, -0.1294095225512604)
+
+FLOPS = 2 * BATCH * TOKENS * WIDTH * 2 * CHANNELS
+
+POW2_SHIFTS = [2**i for i in range(SCALES) if 2**i < TOKENS]
+TRIPLE_SHIFTS = [3 * 2**j for j in range(SCALES) if 3 * 2**j < TOKENS]
+TERMS = sorted(
+    [(s, i) for i, s in enumerate(POW2_SHIFTS)]
+    + [(s, len(POW2_SHIFTS) + j) for j, s in enumerate(TRIPLE_SHIFTS)]
+)
+POOL_MIN_SHIFT = 48
+VECTOR_TERMS = [term for term in TERMS if term[0] < POOL_MIN_SHIFT]
+POOL_TERMS = [term for term in TERMS if term[0] >= POOL_MIN_SHIFT]
+
+
+ROUNDS = max(len(VECTOR_TERMS), len(POOL_TERMS))
+JOIN_ROUND = 2
+
+
+def turn(nc, turned, rows_bf16, pair, ident_f32):
+    words = rows_bf16.bitcast(F32)
+    for u in range(2):
+        for a in range(2):
+            nc.tensor.transpose(
+                turned[:, u, a * P : (a + 1) * P],
+                words[:, 2 * pair + a, u : 2 * P : 2],
+                ident_f32,
+            )
+
+
+def regroup(copy, turned, pair, grouped):
+    copy(
+        out=grouped.bitcast(F32)[:, 2 * pair * P : 2 * (pair + 1) * P, :],
+        in_=turned.rearrange("p u c -> p c u"),
+    )
+
+
+def quantise(nc, grouped, codes, scales):
+    nc.vector.quantize_mx(
+        out=codes.bitcast(FP8X4), scales=scales, in_=grouped.rearrange("p c t -> p (c t)")
+    )
+
+
+def tile_causalwaveletfieldattentionbyte_pa_s_kernel(
+    tc, x, k_w, k_b, v_w, v_b, scale_gain, out
+):
+    nc = tc.nc
+    with ExitStack() as stack:
+        const = stack.enter_context(tc.tile_pool(name="const", bufs=1))
+        per_batch = stack.enter_context(tc.tile_pool(name="per_batch", bufs=BATCH))
+        planes = stack.enter_context(tc.tile_pool(name="planes", bufs=3))
+        work = stack.enter_context(tc.psum_pool(name="work", bufs=4))
+        field_banks = stack.enter_context(tc.psum_pool(name="field_banks", bufs=1))
+        stack.enter_context(tc.manual_schedule())
+
+        def work_bank(shape, name):
+            return work.tile(shape, F32, name=name, tag="work")
+
+        def field_bank(shape, dtype, name, b, h):
+            return field_banks.tile(shape, dtype, name=name, tag="field_%d_%d" % (b, h))
+
+        logits_padded = const.tile([P, HALVES, 16], BF16, name="logits_padded")
+        nc.vector.memset(logits_padded[:], 0.0)
+        logits = logits_padded[:, :, 0:SCALES]
+        with nc.allow_non_contiguous_dma(reason="160 logits, ten to each head's first channel"):
+            for h in range(HALVES):
+                nc.scalar.dma_start(
+                    out=logits[0:P:HEAD_DIM, h, :],
+                    in_=scale_gain[:, h * HEADS_PER_HALF : (h + 1) * HEADS_PER_HALF].rearrange("j i -> i j"),
+                )
+        bias_rows = const.tile([P, P], BF16, name="bias_rows")
+        nc.vector.memset(bias_rows[:], 0.0)
+        nc.scalar.dma_start(out=bias_rows[0:2, :], in_=k_b.rearrange("(a c) -> a c", c=P))
+        nc.scalar.dma_start(out=bias_rows[2:4, :], in_=v_b.rearrange("(a c) -> a c", c=P))
+        table_warm = const.tile([P, 1], F32, name="table_warm")
+        nc.vector.memset(table_warm[:], 1.0)
+        nc.scalar.activation(out=table_warm[:], in_=table_warm[:], func=ACT.Exp)
+
+        x_rows = [
+            const.tile([P, TOKEN_BLOCKS, WIDTH], BF16, name="x_rows_%d" % b) for b in range(BATCH)
+        ]
+        w_rows = const.tile([P, 4, WIDTH], BF16, name="w_rows")
+        x0_blocks = x[0].rearrange("(a p) d -> p a d", p=P)
+        nc.sync.dma_start(out=x_rows[0][:, 0:2, :], in_=x0_blocks[:, 0:2, :])
+        nc.sync.dma_start(out=x_rows[0][:, 2:4, :], in_=x0_blocks[:, 2:4, :])
+        nc.sync.dma_start(out=w_rows[:, 0:2, :], in_=k_w.rearrange("(a p) d -> p a d", p=P))
+        nc.sync.dma_start(out=w_rows[:, 2:4, :], in_=v_w.rearrange("(a p) d -> p a d", p=P))
+        nc.sync.dma_start(out=x_rows[1][:], in_=x[1].rearrange("(a p) d -> p a d", p=P))
+
+        ident_f32 = const.tile([P, P], F32, name="ident_f32")
+        make_identity(nc, ident_f32[:])
+        ident_bf16 = const.tile([P, P], BF16, name="ident_bf16")
+        nc.vector.tensor_copy(out=ident_bf16[:], in_=ident_f32[:])
+        head_of = const.tile([P, HEADS_PER_HALF], F32, name="head_of")
+        nc.vector.tensor_reduce(
+            out=head_of[:],
+            in_=ident_f32[:].rearrange("p (i c) -> p i c", c=HEAD_DIM),
+            axis=AXIS.X,
+            op=ALU.add,
+        )
+        same_head = const.tile([P, HEADS_PER_HALF, HEAD_DIM], F32, name="same_head")
+        nc.vector.tensor_copy(
+            out=same_head[:],
+            in_=head_of[:].unsqueeze(2).to_broadcast([P, HEADS_PER_HALF, HEAD_DIM]),
+        )
+        is_first = const.tile([P, 1], F32, name="is_first")
+        nc.vector.tensor_reduce(out=is_first[:], in_=ident_f32[:, 0:P:HEAD_DIM], axis=AXIS.X, op=ALU.add)
+        spread = const.tile([P, P], F32, name="spread")
+        nc.vector.tensor_scalar_mul(
+            out=spread[:], in0=same_head[:].rearrange("p i c -> p (i c)"), scalar1=is_first[:, 0:1]
+        )
+
+        x_grouped = [
+            const.tile([P, TOKENS, 4], BF16, name="x_grouped_%d" % b, align_bytes=64) for b in range(BATCH)
+        ]
+        x_codes = [const.tile([P, TOKENS], U32, name="x_codes_%d" % b, align_bytes=64) for b in range(BATCH)]
+        x_scales = [const.tile([P, TOKENS], U8, name="x_scales_%d" % b, align_bytes=64) for b in range(BATCH)]
+        w_grouped = const.tile([P, 2 * CHANNELS, 4], BF16, name="w_grouped", align_bytes=64)
+        w_codes = const.tile([P, 2 * CHANNELS], U32, name="w_codes", align_bytes=64)
+        w_scales = const.tile([P, 2 * CHANNELS], U8, name="w_scales", align_bytes=64)
+        k_cols, v_cols = slice(0, CHANNELS), slice(CHANNELS, 2 * CHANNELS)
+        turned_shape = [P, 2, 2 * P]
+
+        for pair, copy in ((0, nc.vector.tensor_copy), (1, nc.scalar.copy)):
+            turned = work_bank(turned_shape, "turned")
+            turn(nc, turned[:], x_rows[0][:], pair, ident_f32[:])
+            regroup(copy, turned[:], pair, x_grouped[0][:])
+
+        shape_hj = [P, HALVES, SCALES]
+        minus_top = const.tile([P, HALVES], F32, name="minus_top")
+        nc.vector.tensor_reduce(out=minus_top[:], in_=logits, axis=AXIS.X, op=ALU.max, negate=True)
+        gain = const.tile(shape_hj, F32, name="gain")
+        total = const.tile([P, HALVES, 8], F32, name="total")
+        for h in range(HALVES):
+            nc.scalar.activation(
+                out=gain[:, h, :],
+                in_=logits[:, h, :],
+                func=ACT.Exp,
+                bias=minus_top[:, h : h + 1],
+                scale=1.0,
+                accum_out=total[:, h, 0:1],
+            )
+        nc.scalar.activation(out=table_warm[:], in_=gain[:, 0, 0:1], func=ACT.Sqrt)
+
+        turned = work_bank(turned_shape, "turned")
+        turn(nc, turned[:], w_rows[:], 0, ident_f32[:])
+        regroup(nc.vector.tensor_copy, turned[:], 0, w_grouped[:])
+        quantise(nc, x_grouped[0][:], x_codes[0][:], x_scales[0][:])
+        quantise(nc, w_grouped[:, k_cols, :], w_codes[:, k_cols], w_scales[:, k_cols])
+        turned = work_bank(turned_shape, "turned")
+        turn(nc, turned[:], w_rows[:], 1, ident_f32[:])
+        regroup(nc.vector.tensor_copy, turned[:], 1, w_grouped[:])
+
+        bias_ps = field_bank([P, P], BF16, "bias_ps", 0, 0)
+        nc.tensor.transpose(bias_ps[:], bias_rows[:], ident_bf16[:])
+        bias = const.tile([P, 2, HALVES], F32, name="bias")
+        nc.vector.tensor_copy(out=bias[:].rearrange("p w h -> p (w h)"), in_=bias_ps[:, 0 : 2 * HALVES])
+        quantise(nc, w_grouped[:, v_cols, :], w_codes[:, v_cols], w_scales[:, v_cols])
+
+        turned_late = [field_bank(turned_shape, F32, "turned_late", 1, pair) for pair in range(2)]
+        for pair in range(2):
+            turn(nc, turned_late[pair][:], x_rows[1][:], pair, ident_f32[:])
+
+        tiles = {}
+        for b in range(BATCH):
+            for name in ("k_square", "v_full", "base", "result", "pool_sum"):
+                tiles[(name, b)] = per_batch.tile([P, HALVES, TOKENS], F32, name=name)
+            tiles[("norm", b)] = per_batch.tile([P, HALVES, TOKEN_BLOCKS * HEADS_PER_HALF], F32, name="norm")
+            tiles[("f_tok", b)] = per_batch.tile([P, HALVES, TOKEN_BLOCKS, P], F32, name="f_tok")
+        v_toks = {}
+        fields = {}
+
+        def project(b, which):
+            func, dest = ((ACT.Square, "k_square"), (ACT.Identity, "v_full"))[which]
+            for h in range(HALVES):
+                cols = slice(which * CHANNELS + h * P, which * CHANNELS + (h + 1) * P)
+                proj = work_bank([P, TOKENS], "proj")
+                nc.tensor.matmul_mx(
+                    out=proj[:],
+                    lhsT=w_codes[:, cols].bitcast(FP8X4),
+                    lhsT_scale=w_scales[:, cols],
+                    rhs=x_codes[b][:].bitcast(FP8X4),
+                    rhs_scale=x_scales[b][:],
+                    start=True,
+                    stop=True,
+                )
+                nc.scalar.activation(
+                    out=tiles[(dest, b)][:, h, :], in_=proj[:], func=func, bias=bias[:, which, h : h + 1], scale=1.0
+                )
+
+        def norm(b, h):
+            norm_ps = work_bank([P, TOKEN_BLOCKS, HEADS_PER_HALF], "norm_ps")
+            for a in range(TOKEN_BLOCKS):
+                nc.tensor.matmul(
+                    out=norm_ps[:, a, :],
+                    lhsT=tiles[("k_square", b)][:, h, a * P : (a + 1) * P],
+                    rhs=head_of[:],
+                    start=True,
+                    stop=True,
+                )
+            nc.scalar.activation(
+                out=tiles[("norm", b)][:, h, :], in_=norm_ps[:].rearrange("p a i -> p (a i)"), func=ACT.Sqrt
+            )
+
+        def turn_v(b):
+            for h in range(HALVES):
+                v_tok = work_bank([P, TOKEN_BLOCKS, P], "v_tok")
+                for a in range(TOKEN_BLOCKS):
+                    nc.tensor.transpose(
+                        v_tok[:, a, :], tiles[("v_full", b)][:, h, a * P : (a + 1) * P], ident_f32[:]
+                    )
+                v_toks[(b, h)] = v_tok
+
+        def make_field(b, h):
+            f_tok = tiles[("f_tok", b)]
+            nc.vector.tensor_tensor(
+                out=f_tok[:, h, :, :].rearrange("p a (i c) -> p (a i) c", c=HEAD_DIM),
+                in0=v_toks[(b, h)][:].rearrange("p a (i c) -> p (a i) c", c=HEAD_DIM),
+                in1=tiles[("norm", b)][:, h, :]
+                .unsqueeze(2)
+                .to_broadcast([P, TOKEN_BLOCKS * HEADS_PER_HALF, HEAD_DIM]),
+                op=ALU.mult,
+            )
+            field = field_bank([P, TOKENS], F32, "field", b, h)
+            for a in range(TOKEN_BLOCKS):
+                nc.tensor.transpose(field[:, a * P : (a + 1) * P], f_tok[:, h, a, :], ident_f32[:])
+            fields[(b, h)] = field
+            nc.scalar.activation(out=tiles[("base", b)][:, h, :], in_=field[:], func=ACT.Copy, scale=TAPS[3])
+
+        def stages(b):
+            return [
+                lambda: project(b, 0),
+                lambda: project(b, 1),
+                lambda: norm(b, 0),
+                lambda: norm(b, 1),
+                lambda: turn_v(b),
+                lambda: make_field(b, 0),
+                lambda: make_field(b, 1),
+            ]
+
+        first = stages(0)
+        first[0]()
+        first[1]()
+
+        n_pow2, n_triple = len(POW2_SHIFTS), len(TRIPLE_SHIFTS)
+        table_shape = [P, HALVES, n_pow2 + n_triple]
+        by_head = const.tile(table_shape, F32, name="by_head")
+        nc.vector.reciprocal(out=total[:, :, 0:1], in_=total[:, :, 0:1])
+        regroup(nc.vector.tensor_copy, turned_late[0][:], 0, x_grouped[1][:])
+        nc.vector.tensor_tensor(
+            out=gain[:], in0=gain[:], in1=total[:, :, 0:1].to_broadcast(shape_hj), op=ALU.mult
+        )
+        regroup(nc.vector.tensor_copy, turned_late[1][:], 1, x_grouped[1][:])
+        nc.vector.tensor_scalar_mul(out=by_head[:, :, 0:n_pow2], in0=gain[:, :, 0:n_pow2], scalar1=TAPS[2])
+        nc.vector.tensor_scalar_mul(out=by_head[:, :, n_pow2:], in0=gain[:, :, 0:n_triple], scalar1=TAPS[0])
+        quantise(nc, x_grouped[1][:], x_codes[1][:], x_scales[1][:])
+        nc.vector.scalar_tensor_tensor(
+            out=by_head[:, :, 1:n_pow2],
+            in0=gain[:, :, 0 : n_pow2 - 1],
+            scalar=TAPS[1],
+            in1=by_head[:, :, 1:n_pow2],
+            op0=ALU.mult,
+            op1=ALU.add,
+        )
+
+        for stage in first[2:5]:
+            stage()
+        by_channel_ps = field_bank(table_shape, F32, "by_channel_ps", 1, 0)
+        nc.tensor.matmul(
+            out=by_channel_ps[:].rearrange("p h t -> p (h t)"),
+            lhsT=spread[:],
+            rhs=by_head[:].rearrange("p h t -> p (h t)"),
+            start=True,
+            stop=True,
+        )
+        for stage in first[5:]:
+            stage()
+        coef = const.tile(table_shape, F32, name="coef")
+        nc.vector.tensor_copy(out=coef[:], in_=by_channel_ps[:])
+        coef_over_tap3 = const.tile(table_shape, F32, name="coef_over_tap3")
+        nc.vector.tensor_scalar_mul(out=coef_over_tap3[:], in0=by_channel_ps[:], scalar1=1.0 / TAPS[3])
+
+        def vector_term(b, r):
+            shift, col = VECTOR_TERMS[r]
+            base, result = tiles[("base", b)], tiles[("result", b)]
+            addend = base if r == 0 else result
+            for h in range(HALVES):
+                if r == 0:
+                    nc.vector.tensor_copy(out=result[:, h, 0:shift], in_=base[:, h, 0:shift])
+                nc.vector.scalar_tensor_tensor(
+                    out=result[:, h, shift:],
+                    in0=fields[(b, h)][:, 0 : TOKENS - shift],
+                    scalar=coef[:, h, col : col + 1],
+                    in1=addend[:, h, shift:],
+                    op0=ALU.mult,
+                    op1=ALU.add,
+                )
+
+        def pool_term(b, r):
+            shift, col = POOL_TERMS[r]
+            pool_sum = tiles[("pool_sum", b)]
+            scaled = pool_sum if r == 0 else planes.tile([P, HALVES, TOKENS], F32, name="plane")
+            for h in range(HALVES):
+                nc.scalar.activation(
+                    out=scaled[:, h, shift:],
+                    in_=tiles[("base", b)][:, h, 0 : TOKENS - shift],
+                    func=ACT.Copy,
+                    scale=coef_over_tap3[:, h, col : col + 1],
+                )
+            if r > 0:
+                nc.gpsimd.tensor_tensor(
+                    out=pool_sum[:, :, shift:], in0=pool_sum[:, :, shift:], in1=scaled[:, :, shift:], op=ALU.add
+                )
+
+        def join_and_store(b):
+            first_shift = POOL_TERMS[0][0]
+            result, pool_sum = tiles[("result", b)], tiles[("pool_sum", b)]
+            for h in range(HALVES):
+                nc.vector.tensor_tensor(
+                    out=result[:, h, first_shift:],
+                    in0=result[:, h, first_shift:],
+                    in1=pool_sum[:, h, first_shift:],
+                    op=ALU.add,
+                )
+                nc.sync.dma_start(out=out[b, h * P : (h + 1) * P, :], in_=result[:, h, :])
+
+        for b in range(BATCH):
+            later = stages(b + 1) if b + 1 < BATCH else []
+            for r in range(ROUNDS):
+                if r < len(VECTOR_TERMS):
+                    vector_term(b, r)
+                if r < len(POOL_TERMS):
+                    pool_term(b, r)
+                if 1 <= r <= len(later):
+                    later[r - 1]()
+                if b > 0 and r == JOIN_ROUND:
+                    join_and_store(b - 1)
+        join_and_store(BATCH - 1)

@@ -20,39 +20,32 @@ HEADS_PER_HALF = P // HEAD_DIM
 TOKEN_BLOCKS = TOKENS // P
 TAPS = (0.4829629131445341, 0.8365163037378079, 0.2241438680420134, -0.1294095225512604)
 
+PAD = 4
+CLASSES = 4
+
 FLOPS = 2 * BATCH * TOKENS * WIDTH * 2 * CHANNELS
 
 POW2_SHIFTS = [2**i for i in range(SCALES) if 2**i < TOKENS]
 TRIPLE_SHIFTS = [3 * 2**j for j in range(SCALES) if 3 * 2**j < TOKENS]
-TERMS = sorted(
-    [(s, i) for i, s in enumerate(POW2_SHIFTS)]
-    + [(s, len(POW2_SHIFTS) + j) for j, s in enumerate(TRIPLE_SHIFTS)]
-)
-POOL_MIN_SHIFT = 48
-VECTOR_TERMS = [term for term in TERMS if term[0] < POOL_MIN_SHIFT]
-POOL_TERMS = [term for term in TERMS if term[0] >= POOL_MIN_SHIFT]
+N_POW2, N_TRIPLE = len(POW2_SHIFTS), len(TRIPLE_SHIFTS)
+COLUMN = {s: i for i, s in enumerate(POW2_SHIFTS + TRIPLE_SHIFTS)}
+ALL_SHIFTS = sorted(COLUMN)
+ODD_SHIFTS = [s for s in ALL_SHIFTS if s % CLASSES]
+POOL_MIN_SHIFT = 24
+VECTOR_SHIFTS = [s for s in ALL_SHIFTS if s < POOL_MIN_SHIFT]
+POOL_SHIFTS = [s for s in ALL_SHIFTS if s >= POOL_MIN_SHIFT]
+ROW, ORIGIN = 2 * P, P - 1
 
 
-ROUNDS = max(len(VECTOR_TERMS), len(POOL_TERMS))
-JOIN_ROUND = 2
-
-
-def turn(nc, turned, rows_bf16, pair, ident_f32):
+def turn(nc, turned, rows_bf16, blocks, ident_f32):
     words = rows_bf16.bitcast(F32)
-    for u in range(2):
-        for a in range(2):
-            nc.tensor.transpose(
-                turned[:, u, a * P : (a + 1) * P],
-                words[:, 2 * pair + a, u : 2 * P : 2],
-                ident_f32,
-            )
+    for i, a in enumerate(blocks):
+        for u in range(2):
+            nc.tensor.transpose(turned[:, u, i * P : (i + 1) * P], words[:, a, u : 2 * P : 2], ident_f32)
 
 
-def regroup(copy, turned, pair, grouped):
-    copy(
-        out=grouped.bitcast(F32)[:, 2 * pair * P : 2 * (pair + 1) * P, :],
-        in_=turned.rearrange("p u c -> p c u"),
-    )
+def regroup(copy, turned, grouped):
+    copy(out=grouped.bitcast(F32), in_=turned.rearrange("p u c -> p c u"))
 
 
 def quantise(nc, grouped, codes, scales):
@@ -67,31 +60,19 @@ def tile_causalwaveletfieldattentionbyte_pa_s_kernel(
     nc = tc.nc
     with ExitStack() as stack:
         const = stack.enter_context(tc.tile_pool(name="const", bufs=1))
-        per_batch = stack.enter_context(tc.tile_pool(name="per_batch", bufs=BATCH))
-        planes = stack.enter_context(tc.tile_pool(name="planes", bufs=3))
-        work = stack.enter_context(tc.psum_pool(name="work", bufs=4))
-        field_banks = stack.enter_context(tc.psum_pool(name="field_banks", bufs=1))
+        stage = stack.enter_context(tc.tile_pool(name="stage", bufs=2))
+        planes = stack.enter_context(tc.tile_pool(name="planes", bufs=8))
+        banks = stack.enter_context(tc.psum_pool(name="banks", bufs=1))
         stack.enter_context(tc.manual_schedule())
 
-        def work_bank(shape, name):
-            return work.tile(shape, F32, name=name, tag="work")
+        def bank(i, shape, name, dtype=F32):
+            return banks.tile(shape, dtype, name=name, tag="bank_%d" % i)
 
-        def field_bank(shape, dtype, name, b, h):
-            return field_banks.tile(shape, dtype, name=name, tag="field_%d_%d" % (b, h))
-
-        logits_padded = const.tile([P, HALVES, 16], BF16, name="logits_padded")
-        nc.vector.memset(logits_padded[:], 0.0)
-        logits = logits_padded[:, :, 0:SCALES]
-        with nc.allow_non_contiguous_dma(reason="160 logits, ten to each head's first channel"):
-            for h in range(HALVES):
-                nc.scalar.dma_start(
-                    out=logits[0:P:HEAD_DIM, h, :],
-                    in_=scale_gain[:, h * HEADS_PER_HALF : (h + 1) * HEADS_PER_HALF].rearrange("j i -> i j"),
-                )
-        bias_rows = const.tile([P, P], BF16, name="bias_rows")
-        nc.vector.memset(bias_rows[:], 0.0)
-        nc.scalar.dma_start(out=bias_rows[0:2, :], in_=k_b.rearrange("(a c) -> a c", c=P))
-        nc.scalar.dma_start(out=bias_rows[2:4, :], in_=v_b.rearrange("(a c) -> a c", c=P))
+        small_rows = const.tile([P, P], BF16, name="small_rows")
+        nc.gpsimd.memset(small_rows[:], 0.0)
+        nc.scalar.dma_start(out=small_rows[4 : 4 + SCALES, 0:HEADS], in_=scale_gain)
+        nc.scalar.dma_start(out=small_rows[0:2, :], in_=k_b.rearrange("(a c) -> a c", c=P))
+        nc.scalar.dma_start(out=small_rows[2:4, :], in_=v_b.rearrange("(a c) -> a c", c=P))
         table_warm = const.tile([P, 1], F32, name="table_warm")
         nc.vector.memset(table_warm[:], 1.0)
         nc.scalar.activation(out=table_warm[:], in_=table_warm[:], func=ACT.Exp)
@@ -111,6 +92,8 @@ def tile_causalwaveletfieldattentionbyte_pa_s_kernel(
         make_identity(nc, ident_f32[:])
         ident_bf16 = const.tile([P, P], BF16, name="ident_bf16")
         nc.vector.tensor_copy(out=ident_bf16[:], in_=ident_f32[:])
+        ones = const.tile([P, P], F32, name="ones")
+        nc.vector.memset(ones[:], 1.0)
         head_of = const.tile([P, HEADS_PER_HALF], F32, name="head_of")
         nc.vector.tensor_reduce(
             out=head_of[:],
@@ -118,17 +101,12 @@ def tile_causalwaveletfieldattentionbyte_pa_s_kernel(
             axis=AXIS.X,
             op=ALU.add,
         )
-        same_head = const.tile([P, HEADS_PER_HALF, HEAD_DIM], F32, name="same_head")
+        spread = const.tile([P, HEADS, HEAD_DIM], F32, name="spread")
         nc.vector.tensor_copy(
-            out=same_head[:],
-            in_=head_of[:].unsqueeze(2).to_broadcast([P, HEADS_PER_HALF, HEAD_DIM]),
+            out=spread[:], in_=ident_f32[:, 0:HEADS].unsqueeze(2).to_broadcast([P, HEADS, HEAD_DIM])
         )
-        is_first = const.tile([P, 1], F32, name="is_first")
-        nc.vector.tensor_reduce(out=is_first[:], in_=ident_f32[:, 0:P:HEAD_DIM], axis=AXIS.X, op=ALU.add)
-        spread = const.tile([P, P], F32, name="spread")
-        nc.vector.tensor_scalar_mul(
-            out=spread[:], in0=same_head[:].rearrange("p i c -> p (i c)"), scalar1=is_first[:, 0:1]
-        )
+        filter_rows = const.tile([P, HEADS_PER_HALF, ROW], F32, name="filter_rows")
+        nc.gpsimd.memset(filter_rows[:], 0.0)
 
         x_grouped = [
             const.tile([P, TOKENS, 4], BF16, name="x_grouped_%d" % b, align_bytes=64) for b in range(BATCH)
@@ -138,221 +116,426 @@ def tile_causalwaveletfieldattentionbyte_pa_s_kernel(
         w_grouped = const.tile([P, 2 * CHANNELS, 4], BF16, name="w_grouped", align_bytes=64)
         w_codes = const.tile([P, 2 * CHANNELS], U32, name="w_codes", align_bytes=64)
         w_scales = const.tile([P, 2 * CHANNELS], U8, name="w_scales", align_bytes=64)
-        k_cols, v_cols = slice(0, CHANNELS), slice(CHANNELS, 2 * CHANNELS)
-        turned_shape = [P, 2, 2 * P]
 
-        for pair, copy in ((0, nc.vector.tensor_copy), (1, nc.scalar.copy)):
-            turned = work_bank(turned_shape, "turned")
-            turn(nc, turned[:], x_rows[0][:], pair, ident_f32[:])
-            regroup(copy, turned[:], pair, x_grouped[0][:])
+        def turned_bank(i, rows, blocks):
+            turned = bank(i, [P, 2, len(blocks) * P], "turned")
+            turn(nc, turned[:], rows[:], blocks, ident_f32[:])
+            return turned[:]
 
-        shape_hj = [P, HALVES, SCALES]
-        minus_top = const.tile([P, HALVES], F32, name="minus_top")
-        nc.vector.tensor_reduce(out=minus_top[:], in_=logits, axis=AXIS.X, op=ALU.max, negate=True)
-        gain = const.tile(shape_hj, F32, name="gain")
-        total = const.tile([P, HALVES, 8], F32, name="total")
-        for h in range(HALVES):
-            nc.scalar.activation(
-                out=gain[:, h, :],
-                in_=logits[:, h, :],
-                func=ACT.Exp,
-                bias=minus_top[:, h : h + 1],
-                scale=1.0,
-                accum_out=total[:, h, 0:1],
+        def quantise_x(b, first, last):
+            cols = slice(first, last)
+            quantise(nc, x_grouped[b][:, cols, :], x_codes[b][:, cols], x_scales[b][:, cols])
+
+        def quantise_w(first, last):
+            cols = slice(first, last)
+            quantise(nc, w_grouped[:, cols, :], w_codes[:, cols], w_scales[:, cols])
+
+        units = [(b, h) for b in range(BATCH) for h in range(HALVES)]
+        k_banks, v_banks, squares, v_full, norm_banks, norms = {}, {}, {}, {}, {}, {}
+        v_toks, f_toks, field_banks, fields = {}, {}, {}, {}
+
+        def project(u, which, i):
+            b, h = units[u]
+            cols = slice(which * CHANNELS + h * P, which * CHANNELS + (h + 1) * P)
+            proj = bank(i, [P, TOKENS], "proj")
+            nc.tensor.matmul_mx(
+                out=proj[:],
+                lhsT=w_codes[:, cols].bitcast(FP8X4),
+                lhsT_scale=w_scales[:, cols],
+                rhs=x_codes[b][:].bitcast(FP8X4),
+                rhs_scale=x_scales[b][:],
+                start=True,
+                stop=True,
             )
-        nc.scalar.activation(out=table_warm[:], in_=gain[:, 0, 0:1], func=ACT.Sqrt)
+            return proj
 
-        turned = work_bank(turned_shape, "turned")
-        turn(nc, turned[:], w_rows[:], 0, ident_f32[:])
-        regroup(nc.vector.tensor_copy, turned[:], 0, w_grouped[:])
-        quantise(nc, x_grouped[0][:], x_codes[0][:], x_scales[0][:])
-        quantise(nc, w_grouped[:, k_cols, :], w_codes[:, k_cols], w_scales[:, k_cols])
-        turned = work_bank(turned_shape, "turned")
-        turn(nc, turned[:], w_rows[:], 1, ident_f32[:])
-        regroup(nc.vector.tensor_copy, turned[:], 1, w_grouped[:])
+        def project_k(u, i):
+            k_banks[u] = project(u, 0, i)
 
-        bias_ps = field_bank([P, P], BF16, "bias_ps", 0, 0)
-        nc.tensor.transpose(bias_ps[:], bias_rows[:], ident_bf16[:])
-        bias = const.tile([P, 2, HALVES], F32, name="bias")
-        nc.vector.tensor_copy(out=bias[:].rearrange("p w h -> p (w h)"), in_=bias_ps[:, 0 : 2 * HALVES])
-        quantise(nc, w_grouped[:, v_cols, :], w_codes[:, v_cols], w_scales[:, v_cols])
+        def project_v(u, i):
+            v_banks[u] = project(u, 1, i)
 
-        turned_late = [field_bank(turned_shape, F32, "turned_late", 1, pair) for pair in range(2)]
-        for pair in range(2):
-            turn(nc, turned_late[pair][:], x_rows[1][:], pair, ident_f32[:])
+        def by_block(u, tile):
+            if units[u][1] == 0:
+                return tile.rearrange("p (a m) -> p a m", m=P)
+            return tile.rearrange("p (m r) -> p r m", r=CLASSES)
 
-        tiles = {}
-        for b in range(BATCH):
-            for name in ("k_square", "v_full", "base", "result", "pool_sum"):
-                tiles[(name, b)] = per_batch.tile([P, HALVES, TOKENS], F32, name=name)
-            tiles[("norm", b)] = per_batch.tile([P, HALVES, TOKEN_BLOCKS * HEADS_PER_HALF], F32, name="norm")
-            tiles[("f_tok", b)] = per_batch.tile([P, HALVES, TOKEN_BLOCKS, P], F32, name="f_tok")
-        v_toks = {}
-        fields = {}
+        def square(u):
+            h = units[u][1]
+            squares[u] = stage.tile([P, TOKEN_BLOCKS, P], F32, name="k_square")
+            nc.scalar.activation(
+                out=squares[u][:],
+                in_=by_block(u, k_banks[u][:]),
+                func=ACT.Square,
+                bias=bias[:, 0, h : h + 1],
+                scale=1.0,
+            )
 
-        def project(b, which):
-            func, dest = ((ACT.Square, "k_square"), (ACT.Identity, "v_full"))[which]
-            for h in range(HALVES):
-                cols = slice(which * CHANNELS + h * P, which * CHANNELS + (h + 1) * P)
-                proj = work_bank([P, TOKENS], "proj")
-                nc.tensor.matmul_mx(
-                    out=proj[:],
-                    lhsT=w_codes[:, cols].bitcast(FP8X4),
-                    lhsT_scale=w_scales[:, cols],
-                    rhs=x_codes[b][:].bitcast(FP8X4),
-                    rhs_scale=x_scales[b][:],
-                    start=True,
-                    stop=True,
-                )
-                nc.scalar.activation(
-                    out=tiles[(dest, b)][:, h, :], in_=proj[:], func=func, bias=bias[:, which, h : h + 1], scale=1.0
-                )
+        def add_v_bias(u):
+            h = units[u][1]
+            v_full[u] = stage.tile([P, TOKEN_BLOCKS, P], F32, name="v_full")
+            nc.scalar.activation(
+                out=v_full[u][:],
+                in_=by_block(u, v_banks[u][:]),
+                func=ACT.Identity,
+                bias=bias[:, 1, h : h + 1],
+                scale=1.0,
+            )
 
-        def norm(b, h):
-            norm_ps = work_bank([P, TOKEN_BLOCKS, HEADS_PER_HALF], "norm_ps")
+        def add_squares(u, i):
+            norm_banks[u] = bank(i, [P, TOKEN_BLOCKS, HEADS_PER_HALF], "norm_ps")
             for a in range(TOKEN_BLOCKS):
                 nc.tensor.matmul(
-                    out=norm_ps[:, a, :],
-                    lhsT=tiles[("k_square", b)][:, h, a * P : (a + 1) * P],
-                    rhs=head_of[:],
-                    start=True,
-                    stop=True,
+                    out=norm_banks[u][:, a, :], lhsT=squares[u][:, a, :], rhs=head_of[:], start=True, stop=True
                 )
-            nc.scalar.activation(
-                out=tiles[("norm", b)][:, h, :], in_=norm_ps[:].rearrange("p a i -> p (a i)"), func=ACT.Sqrt
-            )
 
-        def turn_v(b):
-            for h in range(HALVES):
-                v_tok = work_bank([P, TOKEN_BLOCKS, P], "v_tok")
-                for a in range(TOKEN_BLOCKS):
-                    nc.tensor.transpose(
-                        v_tok[:, a, :], tiles[("v_full", b)][:, h, a * P : (a + 1) * P], ident_f32[:]
-                    )
-                v_toks[(b, h)] = v_tok
+        def root(u):
+            norms[u] = stage.tile([P, TOKEN_BLOCKS, HEADS_PER_HALF], F32, name="norm")
+            nc.scalar.activation(out=norms[u][:], in_=norm_banks[u][:], func=ACT.Sqrt)
 
-        def make_field(b, h):
-            f_tok = tiles[("f_tok", b)]
+        def turn_v(u, i):
+            v_toks[u] = bank(i, [P, TOKEN_BLOCKS, P], "v_tok")
+            for a in range(TOKEN_BLOCKS):
+                nc.tensor.transpose(v_toks[u][:, a, :], v_full[u][:, a, :], ident_f32[:])
+
+        def make_field(u):
+            f_toks[u] = const.tile([P, TOKEN_BLOCKS, P], F32, name="f_tok_%d" % u)
             nc.vector.tensor_tensor(
-                out=f_tok[:, h, :, :].rearrange("p a (i c) -> p (a i) c", c=HEAD_DIM),
-                in0=v_toks[(b, h)][:].rearrange("p a (i c) -> p (a i) c", c=HEAD_DIM),
-                in1=tiles[("norm", b)][:, h, :]
+                out=f_toks[u][:].rearrange("p a (i c) -> p (a i) c", c=HEAD_DIM),
+                in0=v_toks[u][:].rearrange("p a (i c) -> p (a i) c", c=HEAD_DIM),
+                in1=norms[u][:]
+                .rearrange("p a i -> p (a i)")
                 .unsqueeze(2)
                 .to_broadcast([P, TOKEN_BLOCKS * HEADS_PER_HALF, HEAD_DIM]),
                 op=ALU.mult,
             )
-            field = field_bank([P, TOKENS], F32, "field", b, h)
+
+        def turn_field(u, i):
+            field_banks[u] = bank(i, [P, TOKEN_BLOCKS, P], "field_ps")
             for a in range(TOKEN_BLOCKS):
-                nc.tensor.transpose(field[:, a * P : (a + 1) * P], f_tok[:, h, a, :], ident_f32[:])
-            fields[(b, h)] = field
-            nc.scalar.activation(out=tiles[("base", b)][:, h, :], in_=field[:], func=ACT.Copy, scale=TAPS[3])
+                nc.tensor.transpose(field_banks[u][:, a, :], f_toks[u][:, a, :], ident_f32[:])
 
-        def stages(b):
-            return [
-                lambda: project(b, 0),
-                lambda: project(b, 1),
-                lambda: norm(b, 0),
-                lambda: norm(b, 1),
-                lambda: turn_v(b),
-                lambda: make_field(b, 0),
-                lambda: make_field(b, 1),
-            ]
+        def copy_field(u):
+            natural = fields[u][:, PAD:]
+            if units[u][1] == 0:
+                nc.scalar.activation(
+                    out=natural, in_=field_banks[u][:].rearrange("p a m -> p (a m)"), func=ACT.Copy, scale=TAPS[3]
+                )
+            else:
+                nc.scalar.copy(
+                    out=natural.rearrange("p (m r) -> p m r", r=CLASSES),
+                    in_=field_banks[u][:].rearrange("p r m -> p m r"),
+                )
 
-        first = stages(0)
-        first[0]()
-        first[1]()
+        for u in range(len(units)):
+            fields[u] = const.tile([P, PAD + TOKENS], F32, name="field_%d" % u)
+            nc.gpsimd.memset(fields[u][:, 0:PAD], 0.0)
 
-        n_pow2, n_triple = len(POW2_SHIFTS), len(TRIPLE_SHIFTS)
-        table_shape = [P, HALVES, n_pow2 + n_triple]
-        by_head = const.tile(table_shape, F32, name="by_head")
-        nc.vector.reciprocal(out=total[:, :, 0:1], in_=total[:, :, 0:1])
-        regroup(nc.vector.tensor_copy, turned_late[0][:], 0, x_grouped[1][:])
-        nc.vector.tensor_tensor(
-            out=gain[:], in0=gain[:], in1=total[:, :, 0:1].to_broadcast(shape_hj), op=ALU.mult
+        x0_turned = [turned_bank(0, x_rows[0], (0, 1))]
+        small_ps = bank(7, [P, P], "small_ps", BF16)
+        nc.tensor.transpose(small_ps[:], small_rows[:], ident_bf16[:])
+        x0_turned.append(turned_bank(1, x_rows[0], (2, 3)))
+        w0_turned = [turned_bank(2, w_rows, (0,)), turned_bank(3, w_rows, (2,))]
+        w1_turned = turned_bank(4, w_rows, (1, 3))
+        regroup(nc.vector.tensor_copy, x0_turned[0], x_grouped[0][:, 0 : 2 * P, :])
+        regroup(nc.scalar.copy, x0_turned[1], x_grouped[0][:, 2 * P :, :])
+
+        logits = small_ps[:, 4 : 4 + SCALES]
+        minus_top = const.tile([P, 1], F32, name="minus_top")
+        nc.vector.tensor_reduce(out=minus_top[:], in_=logits, axis=AXIS.X, op=ALU.max, negate=True)
+        bias = const.tile([P, 2, HALVES], F32, name="bias")
+        nc.vector.tensor_copy(out=bias[:].rearrange("p w h -> p (w h)"), in_=small_ps[:, 0 : 2 * HALVES])
+        gain = const.tile([P, SCALES], F32, name="gain")
+        total = const.tile([P, 1], F32, name="total")
+        nc.scalar.activation(
+            out=gain[:], in_=logits, func=ACT.Exp, bias=minus_top[:, 0:1], scale=1.0, accum_out=total[:]
         )
-        regroup(nc.vector.tensor_copy, turned_late[1][:], 1, x_grouped[1][:])
-        nc.vector.tensor_scalar_mul(out=by_head[:, :, 0:n_pow2], in0=gain[:, :, 0:n_pow2], scalar1=TAPS[2])
-        nc.vector.tensor_scalar_mul(out=by_head[:, :, n_pow2:], in0=gain[:, :, 0:n_triple], scalar1=TAPS[0])
-        quantise(nc, x_grouped[1][:], x_codes[1][:], x_scales[1][:])
+        nc.scalar.activation(out=table_warm[:], in_=ones[:, 0:1], func=ACT.Sqrt)
+
+        def regroup_w(copy, turned, which):
+            first = which * CHANNELS
+            regroup(copy, turned, w_grouped[:, first : first + P, :])
+
+        quantise_x(0, 0, 2 * P)
+        regroup_w(nc.vector.tensor_copy, w0_turned[0], 0)
+        quantise_x(0, 2 * P, TOKENS)
+        quantise_w(0, P)
+        project_k(0, 0)
+        regroup_w(nc.vector.tensor_copy, w0_turned[1], 1)
+
+        quantise_w(CHANNELS, CHANNELS + P)
+        project_v(0, 1)
+        x1_turned = [turned_bank(5, x_rows[1], (0, 1))]
+        square(0)
+        nc.vector.reciprocal(out=total[:], in_=total[:])
+        add_v_bias(0)
+        nc.vector.tensor_scalar_mul(out=gain[:], in0=gain[:], scalar1=total[:, 0:1])
+        nc.vector.tensor_copy(
+            out=w_grouped[:].bitcast(F32).rearrange("p (w h c) u -> p w h c u", w=2, h=HALVES)[:, :, 1, :, :],
+            in_=w1_turned.rearrange("p u (w c) -> p w c u", w=2),
+        )
+        by_head = const.tile([P, N_POW2 + N_TRIPLE], F32, name="by_head")
+        nc.vector.tensor_scalar_mul(out=by_head[:, 0:N_POW2], in0=gain[:, 0:N_POW2], scalar1=TAPS[2])
+        nc.vector.tensor_scalar_mul(out=by_head[:, N_POW2:], in0=gain[:, 0:N_TRIPLE], scalar1=TAPS[0])
+        quantise_w(P, CHANNELS)
         nc.vector.scalar_tensor_tensor(
-            out=by_head[:, :, 1:n_pow2],
-            in0=gain[:, :, 0 : n_pow2 - 1],
+            out=by_head[:, 1:N_POW2],
+            in0=gain[:, 0 : N_POW2 - 1],
             scalar=TAPS[1],
-            in1=by_head[:, :, 1:n_pow2],
+            in1=by_head[:, 1:N_POW2],
             op0=ALU.mult,
             op1=ALU.add,
         )
-
-        for stage in first[2:5]:
-            stage()
-        by_channel_ps = field_bank(table_shape, F32, "by_channel_ps", 1, 0)
+        first_pow2, first_triple = POW2_SHIFTS.index(CLASSES), TRIPLE_SHIFTS.index(3 * CLASSES)
+        n_pow2, n_triple = N_POW2 - first_pow2, N_TRIPLE - first_triple
+        apart = const.tile([P, HEADS_PER_HALF, n_pow2 + n_triple], F32, name="apart")
+        for dest, first, count in (
+            (apart[:, :, 0:n_pow2], first_pow2, n_pow2),
+            (apart[:, :, n_pow2:], N_POW2 + first_triple, n_triple),
+        ):
+            shape = [P, HEADS_PER_HALF, count]
+            nc.gpsimd.tensor_tensor(
+                out=dest,
+                in0=ident_f32[:, HEADS_PER_HALF:HEADS].unsqueeze(2).to_broadcast(shape),
+                in1=by_head[:, first : first + count].unsqueeze(1).to_broadcast(shape),
+                op=ALU.mult,
+            )
+        add_squares(0, 2)
+        root(0)
+        turn_v(0, 3)
+        by_channel_ps = bank(7, [P, HALVES, N_POW2 + N_TRIPLE], "by_channel_ps")
+        for h in range(HALVES):
+            nc.tensor.matmul(
+                out=by_channel_ps[:, h, :],
+                lhsT=spread[:].rearrange("p i c -> p (i c)")[:, h * P : (h + 1) * P],
+                rhs=by_head[:],
+                start=True,
+                stop=True,
+            )
+        x1_turned.append(turned_bank(6, x_rows[1], (2, 3)))
+        regroup(nc.vector.tensor_copy, x1_turned[0], x_grouped[1][:, 0 : 2 * P, :])
+        make_field(0)
+        turn_field(0, 4)
+        copy_field(0)
+        everywhere = bank(2, [P, HEADS_PER_HALF, n_pow2 + n_triple], "everywhere")
         nc.tensor.matmul(
-            out=by_channel_ps[:].rearrange("p h t -> p (h t)"),
-            lhsT=spread[:],
-            rhs=by_head[:].rearrange("p h t -> p (h t)"),
+            out=everywhere[:].rearrange("p i t -> p (i t)"),
+            lhsT=ones[:],
+            rhs=apart[:].rearrange("p i t -> p (i t)"),
             start=True,
             stop=True,
         )
-        for stage in first[5:]:
-            stage()
-        coef = const.tile(table_shape, F32, name="coef")
+        regroup(nc.vector.tensor_copy, x1_turned[1], x_grouped[1][:, 2 * P :, :])
+        quantise_x(1, 0, 2 * P)
+        quantise_w(CHANNELS + P, 2 * CHANNELS)
+        coef = const.tile([P, HALVES, N_POW2 + N_TRIPLE], F32, name="coef")
         nc.vector.tensor_copy(out=coef[:], in_=by_channel_ps[:])
-        coef_over_tap3 = const.tile(table_shape, F32, name="coef_over_tap3")
-        nc.vector.tensor_scalar_mul(out=coef_over_tap3[:], in0=by_channel_ps[:], scalar1=1.0 / TAPS[3])
+        coef_over_tap3 = const.tile([P, N_POW2 + N_TRIPLE], F32, name="coef_over_tap3")
+        nc.vector.tensor_scalar_mul(out=coef_over_tap3[:], in0=by_channel_ps[:, 0, :], scalar1=1.0 / TAPS[3])
+        quantise_x(1, 2 * P, TOKENS)
+        everywhere_sb = const.tile([P, HEADS_PER_HALF, n_pow2 + n_triple], F32, name="everywhere_sb")
+        nc.vector.tensor_copy(out=everywhere_sb[:], in_=everywhere[:])
+        project_k(2, 0)
+        project_v(2, 1)
 
-        def vector_term(b, r):
-            shift, col = VECTOR_TERMS[r]
-            base, result = tiles[("base", b)], tiles[("result", b)]
-            addend = base if r == 0 else result
-            for h in range(HALVES):
-                if r == 0:
-                    nc.vector.tensor_copy(out=result[:, h, 0:shift], in_=base[:, h, 0:shift])
+        nc.gpsimd.tensor_scalar(
+            out=filter_rows[:, :, ORIGIN : ORIGIN + 1],
+            in0=ones[:, 0:HEADS_PER_HALF].unsqueeze(2),
+            scalar1=TAPS[3],
+            scalar2=0.0,
+            op0=ALU.mult,
+            op1=ALU.add,
+        )
+        for first, count, factor in ((0, n_pow2, 1), (n_pow2, n_triple, 3)):
+            for j in range(0, count, 2):
+                i, n = factor * 2**j, min(2, count - j)
+                nc.gpsimd.tensor_scalar(
+                    out=filter_rows[:, :, ORIGIN + i : ORIGIN + i + (n - 1) * i + 1 : i],
+                    in0=everywhere_sb[:, :, first + j : first + j + n],
+                    scalar1=1.0,
+                    scalar2=0.0,
+                    op0=ALU.mult,
+                    op1=ALU.add,
+                )
+        flat = out.rearrange("b c n -> (b c n)").rearrange("(i k) -> i k", k=P * ROW)
+        nc.sync.dma_start(out=flat.rearrange("i (k l) -> k i l", l=ROW), in_=filter_rows[:])
+        toeplitz = const.tile([P, HEADS_PER_HALF, P], F32, name="toeplitz")
+        nc.sync.dma_start(
+            out=toeplitz[:],
+            in_=flat[:, 0 : P * (ROW - 1)].rearrange("i (k l) -> k i l", l=ROW - 1)[:, :, ORIGIN : ORIGIN + P],
+        )
+
+        results = [const.tile([P, TOKENS], F32, name="result_%d" % u) for u in range(len(units))]
+        pool_sums, long_banks, long_toks, back_banks = {}, {}, {}, {}
+
+        def vector_term(u, r):
+            shift = VECTOR_SHIFTS[r]
+            col = COLUMN[shift]
+            base = fields[u][:, PAD:]
+            if r == 0:
+                nc.vector.tensor_copy(out=results[u][:, 0:shift], in_=base[:, 0:shift])
+            for first, last in ((shift, TOKENS // 2), (TOKENS // 2, TOKENS)):
                 nc.vector.scalar_tensor_tensor(
-                    out=result[:, h, shift:],
-                    in0=fields[(b, h)][:, 0 : TOKENS - shift],
-                    scalar=coef[:, h, col : col + 1],
-                    in1=addend[:, h, shift:],
+                    out=results[u][:, first:last],
+                    in0=field_banks[u][:].rearrange("p a m -> p (a m)")[:, first - shift : last - shift],
+                    scalar=coef[:, 0, col : col + 1],
+                    in1=(base if r == 0 else results[u])[:, first:last],
                     op0=ALU.mult,
                     op1=ALU.add,
                 )
 
-        def pool_term(b, r):
-            shift, col = POOL_TERMS[r]
-            pool_sum = tiles[("pool_sum", b)]
-            scaled = pool_sum if r == 0 else planes.tile([P, HALVES, TOKENS], F32, name="plane")
-            for h in range(HALVES):
-                nc.scalar.activation(
-                    out=scaled[:, h, shift:],
-                    in_=tiles[("base", b)][:, h, 0 : TOKENS - shift],
-                    func=ACT.Copy,
-                    scale=coef_over_tap3[:, h, col : col + 1],
-                )
+        def pool_term(u, r):
+            shift = POOL_SHIFTS[r]
+            col = COLUMN[shift]
+            if r == 0:
+                pool_sums[u] = stage.tile([P, TOKENS], F32, name="pool_sum")
+            scaled = pool_sums[u] if r == 0 else planes.tile([P, TOKENS], F32, name="plane")
+            nc.scalar.activation(
+                out=scaled[:, shift:],
+                in_=fields[u][:, PAD : PAD + TOKENS - shift],
+                func=ACT.Copy,
+                scale=coef_over_tap3[:, col : col + 1],
+            )
             if r > 0:
                 nc.gpsimd.tensor_tensor(
-                    out=pool_sum[:, :, shift:], in0=pool_sum[:, :, shift:], in1=scaled[:, :, shift:], op=ALU.add
+                    out=pool_sums[u][:, shift:], in0=pool_sums[u][:, shift:], in1=scaled[:, shift:], op=ALU.add
                 )
 
-        def join_and_store(b):
-            first_shift = POOL_TERMS[0][0]
-            result, pool_sum = tiles[("result", b)], tiles[("pool_sum", b)]
-            for h in range(HALVES):
-                nc.vector.tensor_tensor(
-                    out=result[:, h, first_shift:],
-                    in0=result[:, h, first_shift:],
-                    in1=pool_sum[:, h, first_shift:],
-                    op=ALU.add,
-                )
-                nc.sync.dma_start(out=out[b, h * P : (h + 1) * P, :], in_=result[:, h, :])
+        def store(u, part=None):
+            b, h = units[u]
+            cols = slice(0, TOKENS) if part is None else slice(part * TOKENS // 2, (part + 1) * TOKENS // 2)
+            nc.sync.dma_start(out=out[b, h * P : (h + 1) * P, cols], in_=results[u][:, cols])
 
-        for b in range(BATCH):
-            later = stages(b + 1) if b + 1 < BATCH else []
-            for r in range(ROUNDS):
-                if r < len(VECTOR_TERMS):
-                    vector_term(b, r)
-                if r < len(POOL_TERMS):
-                    pool_term(b, r)
-                if 1 <= r <= len(later):
-                    later[r - 1]()
-                if b > 0 and r == JOIN_ROUND:
-                    join_and_store(b - 1)
-        join_and_store(BATCH - 1)
+        def join_and_store(u):
+            first_shift = POOL_SHIFTS[0]
+            nc.vector.tensor_tensor(
+                out=results[u][:, first_shift:],
+                in0=results[u][:, first_shift:],
+                in1=pool_sums[u][:, first_shift:],
+                op=ALU.add,
+            )
+            store(u)
+
+        def filter_classes(u, i):
+            long_banks[u] = bank(i, [P, CLASSES, P], "long_ps")
+            for head in range(HEADS_PER_HALF):
+                cols = slice(head * HEAD_DIM, (head + 1) * HEAD_DIM)
+                nc.tensor.matmul(
+                    out=long_banks[u][:, :, cols],
+                    lhsT=toeplitz[:, head, :],
+                    rhs=f_toks[u][:, :, cols],
+                    start=True,
+                    stop=True,
+                )
+
+        def copy_long(u):
+            long_toks[u] = stage.tile([P, CLASSES, P], F32, name="long_tok")
+            nc.scalar.copy(out=long_toks[u][:], in_=long_banks[u][:])
+
+        def turn_long(u, i):
+            back_banks[u] = bank(i, [P, CLASSES, P], "back_ps")
+            for r in range(CLASSES):
+                nc.tensor.transpose(back_banks[u][:, r, :], long_toks[u][:, r, :], ident_f32[:])
+
+        def odd_term(u, r):
+            shift = ODD_SHIFTS[r]
+            col = COLUMN[shift]
+            scale = coef[:, 1, col : col + 1]
+            if r == 0:
+                nc.vector.tensor_scalar_mul(
+                    out=results[u][:], in0=fields[u][:, PAD - shift : PAD + TOKENS - shift], scalar1=scale
+                )
+                return
+            nc.vector.scalar_tensor_tensor(
+                out=results[u][:, shift:],
+                in0=fields[u][:, PAD : PAD + TOKENS - shift],
+                scalar=scale,
+                in1=results[u][:, shift:],
+                op0=ALU.mult,
+                op1=ALU.add,
+            )
+
+        def add_long_and_store(u):
+            nc.vector.tensor_tensor(
+                out=results[u][:].rearrange("p (m r) -> p m r", r=CLASSES),
+                in0=results[u][:].rearrange("p (m r) -> p m r", r=CLASSES),
+                in1=back_banks[u][:].rearrange("p r m -> p m r"),
+                op=ALU.add,
+            )
+            store(u)
+
+        pool_term(0, 0)
+        pool_term(0, 1)
+        square(2)
+        vector_term(0, 0)
+        add_v_bias(2)
+        add_squares(2, 2)
+        turn_v(2, 3)
+        pool_term(0, 2)
+        vector_term(0, 1)
+        pool_term(0, 3)
+        root(2)
+        project_k(1, 0)
+        project_v(1, 1)
+        pool_term(0, 4)
+        pool_term(0, 5)
+        vector_term(0, 2)
+        vector_term(0, 3)
+        vector_term(0, 4)
+        vector_term(0, 5)
+        make_field(2)
+        turn_field(2, 5)
+        square(1)
+        pool_term(0, 6)
+        copy_field(2)
+        add_v_bias(1)
+        add_squares(1, 2)
+        turn_v(1, 3)
+        pool_term(0, 7)
+        pool_term(0, 8)
+        vector_term(0, 6)
+        vector_term(0, 7)
+        pool_term(2, 0)
+        root(1)
+        pool_term(2, 1)
+        project_k(3, 0)
+        project_v(3, 1)
+        vector_term(2, 0)
+        vector_term(2, 1)
+        make_field(1)
+        turn_field(1, 6)
+        square(3)
+        pool_term(2, 2)
+        vector_term(2, 2)
+        add_v_bias(3)
+        add_squares(3, 2)
+        turn_v(3, 3)
+        filter_classes(1, 0)
+        copy_field(1)
+        root(3)
+        pool_term(2, 3)
+        vector_term(2, 3)
+        pool_term(2, 4)
+        vector_term(2, 4)
+        make_field(3)
+        copy_long(1)
+        turn_long(1, 1)
+        turn_field(3, 6)
+        vector_term(2, 5)
+        filter_classes(3, 0)
+        pool_term(2, 5)
+        copy_field(3)
+        pool_term(2, 6)
+        vector_term(2, 6)
+        join_and_store(0)
+        vector_term(2, 7)
+        pool_term(2, 7)
+        pool_term(2, 8)
+        copy_long(3)
+        turn_long(3, 7)
+        for r in range(len(ODD_SHIFTS)):
+            odd_term(1, r)
+            odd_term(3, r)
+        add_long_and_store(1)
+        join_and_store(2)
+        add_long_and_store(3)

@@ -20,7 +20,6 @@ HEADS_PER_HALF = P // HEAD_DIM
 TOKEN_BLOCKS = TOKENS // P
 TAPS = (0.4829629131445341, 0.8365163037378079, 0.2241438680420134, -0.1294095225512604)
 
-PAD = 4
 CLASSES = 4
 
 FLOPS = 2 * BATCH * TOKENS * WIDTH * 2 * CHANNELS
@@ -211,25 +210,13 @@ def tile_causalwaveletfieldattentionbyte_pa_s_kernel(
             )
 
         def turn_field(u, i):
-            field_banks[u] = bank(i, [P, TOKEN_BLOCKS, P], "field_ps")
+            field_banks[u] = bank(i, [P, TOKENS], "field_ps")
             for a in range(TOKEN_BLOCKS):
-                nc.tensor.transpose(field_banks[u][:, a, :], f_toks[u][:, a, :], ident_f32[:])
+                nc.tensor.transpose(by_block(u, field_banks[u][:])[:, a, :], f_toks[u][:, a, :], ident_f32[:])
 
         def copy_field(u):
-            natural = fields[u][:, PAD:]
-            if units[u][1] == 0:
-                nc.scalar.activation(
-                    out=natural, in_=field_banks[u][:].rearrange("p a m -> p (a m)"), func=ACT.Copy, scale=TAPS[3]
-                )
-            else:
-                nc.scalar.copy(
-                    out=natural.rearrange("p (m r) -> p m r", r=CLASSES),
-                    in_=field_banks[u][:].rearrange("p r m -> p m r"),
-                )
-
-        for u in range(len(units)):
-            fields[u] = const.tile([P, PAD + TOKENS], F32, name="field_%d" % u)
-            nc.gpsimd.memset(fields[u][:, 0:PAD], 0.0)
+            fields[u] = const.tile([P, TOKENS], F32, name="field_%d" % u)
+            nc.scalar.activation(out=fields[u][:], in_=field_banks[u][:], func=ACT.Copy, scale=TAPS[3])
 
         x0_turned = [turned_bank(0, x_rows[0], (0, 1))]
         small_ps = bank(7, [P, P], "small_ps", BF16)
@@ -366,18 +353,20 @@ def tile_causalwaveletfieldattentionbyte_pa_s_kernel(
         )
 
         results = [const.tile([P, TOKENS], F32, name="result_%d" % u) for u in range(len(units))]
+        for u in (1, 3):
+            nc.gpsimd.memset(results[u][:, 0 : ODD_SHIFTS[0]], 0.0)
         pool_sums, long_banks, long_toks, back_banks = {}, {}, {}, {}
 
         def vector_term(u, r):
             shift = VECTOR_SHIFTS[r]
             col = COLUMN[shift]
-            base = fields[u][:, PAD:]
+            base = fields[u]
             if r == 0:
                 nc.vector.tensor_copy(out=results[u][:, 0:shift], in_=base[:, 0:shift])
             for first, last in ((shift, TOKENS // 2), (TOKENS // 2, TOKENS)):
                 nc.vector.scalar_tensor_tensor(
                     out=results[u][:, first:last],
-                    in0=field_banks[u][:].rearrange("p a m -> p (a m)")[:, first - shift : last - shift],
+                    in0=field_banks[u][:, first - shift : last - shift],
                     scalar=coef[:, 0, col : col + 1],
                     in1=(base if r == 0 else results[u])[:, first:last],
                     op0=ALU.mult,
@@ -392,7 +381,7 @@ def tile_causalwaveletfieldattentionbyte_pa_s_kernel(
             scaled = pool_sums[u] if r == 0 else planes.tile([P, TOKENS], F32, name="plane")
             nc.scalar.activation(
                 out=scaled[:, shift:],
-                in_=fields[u][:, PAD : PAD + TOKENS - shift],
+                in_=fields[u][:, 0 : TOKENS - shift],
                 func=ACT.Copy,
                 scale=coef_over_tap3[:, col : col + 1],
             )
@@ -409,6 +398,16 @@ def tile_causalwaveletfieldattentionbyte_pa_s_kernel(
         def join_and_store(u):
             first_shift = POOL_SHIFTS[0]
             nc.vector.tensor_tensor(
+                out=results[u][:, first_shift:],
+                in0=results[u][:, first_shift:],
+                in1=pool_sums[u][:, first_shift:],
+                op=ALU.add,
+            )
+            store(u)
+
+        def join_on_gpsimd_and_store(u):
+            first_shift = POOL_SHIFTS[0]
+            nc.gpsimd.tensor_tensor(
                 out=results[u][:, first_shift:],
                 in0=results[u][:, first_shift:],
                 in1=pool_sums[u][:, first_shift:],
@@ -441,14 +440,13 @@ def tile_causalwaveletfieldattentionbyte_pa_s_kernel(
             shift = ODD_SHIFTS[r]
             col = COLUMN[shift]
             scale = coef[:, 1, col : col + 1]
+            src = field_banks[u][:, 0 : TOKENS - shift]
             if r == 0:
-                nc.vector.tensor_scalar_mul(
-                    out=results[u][:], in0=fields[u][:, PAD - shift : PAD + TOKENS - shift], scalar1=scale
-                )
+                nc.vector.tensor_scalar_mul(out=results[u][:, shift:], in0=src, scalar1=scale)
                 return
             nc.vector.scalar_tensor_tensor(
                 out=results[u][:, shift:],
-                in0=fields[u][:, PAD : PAD + TOKENS - shift],
+                in0=src,
                 scalar=scale,
                 in1=results[u][:, shift:],
                 op0=ALU.mult,
@@ -510,32 +508,30 @@ def tile_causalwaveletfieldattentionbyte_pa_s_kernel(
         add_v_bias(3)
         add_squares(3, 2)
         turn_v(3, 3)
-        filter_classes(1, 0)
-        copy_field(1)
         root(3)
+        join_on_gpsimd_and_store(0)
         pool_term(2, 3)
         vector_term(2, 3)
         pool_term(2, 4)
         vector_term(2, 4)
         make_field(3)
-        copy_long(1)
-        turn_long(1, 1)
-        turn_field(3, 6)
-        vector_term(2, 5)
-        filter_classes(3, 0)
+        turn_field(3, 7)
+        filter_classes(1, 0)
         pool_term(2, 5)
-        copy_field(3)
+        vector_term(2, 5)
         pool_term(2, 6)
         vector_term(2, 6)
-        join_and_store(0)
-        vector_term(2, 7)
+        filter_classes(3, 1)
         pool_term(2, 7)
         pool_term(2, 8)
+        copy_long(1)
+        turn_long(1, 2)
+        vector_term(2, 7)
         copy_long(3)
-        turn_long(3, 7)
+        turn_long(3, 3)
         for r in range(len(ODD_SHIFTS)):
             odd_term(1, r)
             odd_term(3, r)
         add_long_and_store(1)
-        join_and_store(2)
         add_long_and_store(3)
+        join_and_store(2)

@@ -30,9 +30,11 @@ N_POW2, N_TRIPLE = len(POW2_SHIFTS), len(TRIPLE_SHIFTS)
 COLUMN = {s: i for i, s in enumerate(POW2_SHIFTS + TRIPLE_SHIFTS)}
 ALL_SHIFTS = sorted(COLUMN)
 ODD_SHIFTS = [s for s in ALL_SHIFTS if s % CLASSES]
-POOL_MIN_SHIFT = 24
-VECTOR_SHIFTS = [s for s in ALL_SHIFTS if s < POOL_MIN_SHIFT]
-POOL_SHIFTS = [s for s in ALL_SHIFTS if s >= POOL_MIN_SHIFT]
+SCALED_SHIFT = ODD_SHIFTS.pop()
+SCALED_FIRST = -(-SCALED_SHIFT // CLASSES)
+POOL_MIN_SHIFT = {0: 32, 2: 48}
+VECTOR_SHIFTS = {u: [s for s in ALL_SHIFTS if s < first] for u, first in POOL_MIN_SHIFT.items()}
+POOL_SHIFTS = {u: [s for s in ALL_SHIFTS if s >= first] for u, first in POOL_MIN_SHIFT.items()}
 ROW, ORIGIN = 2 * P, P - 1
 
 
@@ -69,9 +71,6 @@ def tile_causalwaveletfieldattentionbyte_pa_s_kernel(
 
         small_rows = const.tile([P, P], BF16, name="small_rows")
         nc.gpsimd.memset(small_rows[:], 0.0)
-        nc.scalar.dma_start(out=small_rows[4 : 4 + SCALES, 0:HEADS], in_=scale_gain)
-        nc.scalar.dma_start(out=small_rows[0:2, :], in_=k_b.rearrange("(a c) -> a c", c=P))
-        nc.scalar.dma_start(out=small_rows[2:4, :], in_=v_b.rearrange("(a c) -> a c", c=P))
         table_warm = const.tile([P, 1], F32, name="table_warm")
         nc.vector.memset(table_warm[:], 1.0)
         nc.scalar.activation(out=table_warm[:], in_=table_warm[:], func=ACT.Exp)
@@ -82,6 +81,9 @@ def tile_causalwaveletfieldattentionbyte_pa_s_kernel(
         w_rows = const.tile([P, 4, WIDTH], BF16, name="w_rows")
         x0_blocks = x[0].rearrange("(a p) d -> p a d", p=P)
         nc.sync.dma_start(out=x_rows[0][:, 0:2, :], in_=x0_blocks[:, 0:2, :])
+        nc.sync.dma_start(out=small_rows[4 : 4 + SCALES, 0:HEADS], in_=scale_gain)
+        nc.sync.dma_start(out=small_rows[0:2, :], in_=k_b.rearrange("(a c) -> a c", c=P))
+        nc.sync.dma_start(out=small_rows[2:4, :], in_=v_b.rearrange("(a c) -> a c", c=P))
         nc.sync.dma_start(out=x_rows[0][:, 2:4, :], in_=x0_blocks[:, 2:4, :])
         nc.sync.dma_start(out=w_rows[:, 0:2, :], in_=k_w.rearrange("(a p) d -> p a d", p=P))
         nc.sync.dma_start(out=w_rows[:, 2:4, :], in_=v_w.rearrange("(a p) d -> p a d", p=P))
@@ -299,11 +301,6 @@ def tile_causalwaveletfieldattentionbyte_pa_s_kernel(
                 start=True,
                 stop=True,
             )
-        x1_turned.append(turned_bank(6, x_rows[1], (2, 3)))
-        regroup(nc.vector.tensor_copy, x1_turned[0], x_grouped[1][:, 0 : 2 * P, :])
-        make_field(0)
-        turn_field(0, 4)
-        copy_field(0)
         everywhere = bank(2, [P, HEADS_PER_HALF, n_pow2 + n_triple], "everywhere")
         nc.tensor.matmul(
             out=everywhere[:].rearrange("p i t -> p (i t)"),
@@ -312,6 +309,24 @@ def tile_causalwaveletfieldattentionbyte_pa_s_kernel(
             start=True,
             stop=True,
         )
+        nc.scalar.activation(
+            out=filter_rows[:, :, ORIGIN : ORIGIN + 1],
+            in_=ones[:, 0:HEADS_PER_HALF].unsqueeze(2),
+            func=ACT.Copy,
+            scale=TAPS[3],
+        )
+        for first, count, factor in ((0, n_pow2, 1), (n_pow2, n_triple, 3)):
+            for j in range(0, count, 2):
+                i, n = factor * 2**j, min(2, count - j)
+                nc.scalar.copy(
+                    out=filter_rows[:, :, ORIGIN + i : ORIGIN + i + (n - 1) * i + 1 : i],
+                    in_=everywhere[:, :, first + j : first + j + n],
+                )
+        x1_turned.append(turned_bank(6, x_rows[1], (2, 3)))
+        regroup(nc.vector.tensor_copy, x1_turned[0], x_grouped[1][:, 0 : 2 * P, :])
+        make_field(0)
+        turn_field(0, 4)
+        copy_field(0)
         regroup(nc.vector.tensor_copy, x1_turned[1], x_grouped[1][:, 2 * P :, :])
         quantise_x(1, 0, 2 * P)
         quantise_w(CHANNELS + P, 2 * CHANNELS)
@@ -320,30 +335,9 @@ def tile_causalwaveletfieldattentionbyte_pa_s_kernel(
         coef_over_tap3 = const.tile([P, N_POW2 + N_TRIPLE], F32, name="coef_over_tap3")
         nc.vector.tensor_scalar_mul(out=coef_over_tap3[:], in0=by_channel_ps[:, 0, :], scalar1=1.0 / TAPS[3])
         quantise_x(1, 2 * P, TOKENS)
-        everywhere_sb = const.tile([P, HEADS_PER_HALF, n_pow2 + n_triple], F32, name="everywhere_sb")
-        nc.vector.tensor_copy(out=everywhere_sb[:], in_=everywhere[:])
         project_k(2, 0)
         project_v(2, 1)
 
-        nc.gpsimd.tensor_scalar(
-            out=filter_rows[:, :, ORIGIN : ORIGIN + 1],
-            in0=ones[:, 0:HEADS_PER_HALF].unsqueeze(2),
-            scalar1=TAPS[3],
-            scalar2=0.0,
-            op0=ALU.mult,
-            op1=ALU.add,
-        )
-        for first, count, factor in ((0, n_pow2, 1), (n_pow2, n_triple, 3)):
-            for j in range(0, count, 2):
-                i, n = factor * 2**j, min(2, count - j)
-                nc.gpsimd.tensor_scalar(
-                    out=filter_rows[:, :, ORIGIN + i : ORIGIN + i + (n - 1) * i + 1 : i],
-                    in0=everywhere_sb[:, :, first + j : first + j + n],
-                    scalar1=1.0,
-                    scalar2=0.0,
-                    op0=ALU.mult,
-                    op1=ALU.add,
-                )
         flat = out.rearrange("b c n -> (b c n)").rearrange("(i k) -> i k", k=P * ROW)
         nc.sync.dma_start(out=flat.rearrange("i (k l) -> k i l", l=ROW), in_=filter_rows[:])
         toeplitz = const.tile([P, HEADS_PER_HALF, P], F32, name="toeplitz")
@@ -353,12 +347,15 @@ def tile_causalwaveletfieldattentionbyte_pa_s_kernel(
         )
 
         results = [const.tile([P, TOKENS], F32, name="result_%d" % u) for u in range(len(units))]
+        scaled_copies = {}
         for u in (1, 3):
             nc.gpsimd.memset(results[u][:, 0 : ODD_SHIFTS[0]], 0.0)
+            scaled_copies[u] = const.tile([P, CLASSES, P], F32, name="scaled_copy_%d" % u)
+            nc.gpsimd.memset(scaled_copies[u][:, :, 0:SCALED_FIRST], 0.0)
         pool_sums, long_banks, long_toks, back_banks = {}, {}, {}, {}
 
         def vector_term(u, r):
-            shift = VECTOR_SHIFTS[r]
+            shift = VECTOR_SHIFTS[u][r]
             col = COLUMN[shift]
             base = fields[u]
             if r == 0:
@@ -374,7 +371,7 @@ def tile_causalwaveletfieldattentionbyte_pa_s_kernel(
                 )
 
         def pool_term(u, r):
-            shift = POOL_SHIFTS[r]
+            shift = POOL_SHIFTS[u][r]
             col = COLUMN[shift]
             if r == 0:
                 pool_sums[u] = stage.tile([P, TOKENS], F32, name="pool_sum")
@@ -396,7 +393,7 @@ def tile_causalwaveletfieldattentionbyte_pa_s_kernel(
             nc.sync.dma_start(out=out[b, h * P : (h + 1) * P, cols], in_=results[u][:, cols])
 
         def join_and_store(u):
-            first_shift = POOL_SHIFTS[0]
+            first_shift = POOL_SHIFTS[u][0]
             nc.vector.tensor_tensor(
                 out=results[u][:, first_shift:],
                 in0=results[u][:, first_shift:],
@@ -406,7 +403,7 @@ def tile_causalwaveletfieldattentionbyte_pa_s_kernel(
             store(u)
 
         def join_on_gpsimd_and_store(u):
-            first_shift = POOL_SHIFTS[0]
+            first_shift = POOL_SHIFTS[u][0]
             nc.gpsimd.tensor_tensor(
                 out=results[u][:, first_shift:],
                 in0=results[u][:, first_shift:],
@@ -414,6 +411,20 @@ def tile_causalwaveletfieldattentionbyte_pa_s_kernel(
                 op=ALU.add,
             )
             store(u)
+
+        def scale_copy(u):
+            col = COLUMN[SCALED_SHIFT]
+            rest = SCALED_FIRST * CLASSES - SCALED_SHIFT
+            for m, cls, src in (
+                (slice(SCALED_FIRST, P), slice(0, CLASSES), slice(rest, TOKENS - SCALED_SHIFT)),
+                (slice(SCALED_FIRST - 1, SCALED_FIRST), slice(CLASSES - rest, CLASSES), slice(0, rest)),
+            ):
+                nc.scalar.activation(
+                    out=scaled_copies[u][:, cls, m],
+                    in_=field_banks[u][:, src].rearrange("p (m r) -> p r m", r=cls.stop - cls.start),
+                    func=ACT.Copy,
+                    scale=coef[:, 1, col : col + 1],
+                )
 
         def filter_classes(u, i):
             long_banks[u] = bank(i, [P, CLASSES, P], "long_ps")
@@ -423,8 +434,17 @@ def tile_causalwaveletfieldattentionbyte_pa_s_kernel(
                     out=long_banks[u][:, :, cols],
                     lhsT=toeplitz[:, head, :],
                     rhs=f_toks[u][:, :, cols],
-                    start=True,
-                    stop=True,
+                    start=head == 0,
+                    stop=False,
+                )
+            for r in range(CLASSES):
+                nc.tensor.matmul(
+                    out=long_banks[u][:, r, :],
+                    lhsT=scaled_copies[u][:, r, :],
+                    rhs=ident_f32[:],
+                    is_transpose=True,
+                    start=False,
+                    stop=r == CLASSES - 1,
                 )
 
         def copy_long(u):
@@ -490,25 +510,27 @@ def tile_causalwaveletfieldattentionbyte_pa_s_kernel(
         add_squares(1, 2)
         turn_v(1, 3)
         pool_term(0, 7)
-        pool_term(0, 8)
         vector_term(0, 6)
         vector_term(0, 7)
+        vector_term(0, 8)
         pool_term(2, 0)
         root(1)
         pool_term(2, 1)
         project_k(3, 0)
         project_v(3, 1)
         vector_term(2, 0)
-        vector_term(2, 1)
         make_field(1)
         turn_field(1, 6)
         square(3)
+        vector_term(2, 1)
         pool_term(2, 2)
         vector_term(2, 2)
         add_v_bias(3)
         add_squares(3, 2)
         turn_v(3, 3)
+        scale_copy(1)
         root(3)
+        filter_classes(1, 0)
         join_on_gpsimd_and_store(0)
         pool_term(2, 3)
         vector_term(2, 3)
@@ -516,22 +538,22 @@ def tile_causalwaveletfieldattentionbyte_pa_s_kernel(
         vector_term(2, 4)
         make_field(3)
         turn_field(3, 7)
-        filter_classes(1, 0)
-        pool_term(2, 5)
         vector_term(2, 5)
-        pool_term(2, 6)
-        vector_term(2, 6)
-        filter_classes(3, 1)
-        pool_term(2, 7)
-        pool_term(2, 8)
         copy_long(1)
         turn_long(1, 2)
+        scale_copy(3)
+        filter_classes(3, 1)
+        pool_term(2, 5)
+        pool_term(2, 6)
+        vector_term(2, 6)
         vector_term(2, 7)
+        vector_term(2, 8)
+        vector_term(2, 9)
         copy_long(3)
         turn_long(3, 3)
         for r in range(len(ODD_SHIFTS)):
             odd_term(1, r)
             odd_term(3, r)
         add_long_and_store(1)
-        add_long_and_store(3)
         join_and_store(2)
+        add_long_and_store(3)

@@ -29,10 +29,10 @@ TRIPLE_SHIFTS = [3 * 2**j for j in range(SCALES) if 3 * 2**j < TOKENS]
 N_POW2, N_TRIPLE = len(POW2_SHIFTS), len(TRIPLE_SHIFTS)
 COLUMN = {s: i for i, s in enumerate(POW2_SHIFTS + TRIPLE_SHIFTS)}
 ALL_SHIFTS = sorted(COLUMN)
-ODD_SHIFTS = [s for s in ALL_SHIFTS if s % CLASSES]
-SCALED_SHIFT = ODD_SHIFTS.pop()
-SCALED_FIRST = -(-SCALED_SHIFT // CLASSES)
-POOL_MIN_SHIFT = {0: 32, 2: 48}
+CLASS_CHANGES = [s for s in ALL_SHIFTS if s % CLASSES]
+ODD_SHIFTS = {1: CLASS_CHANGES[:1], 3: CLASS_CHANGES[:2]}
+SCALED_SHIFTS = {1: CLASS_CHANGES[1:], 3: CLASS_CHANGES[2:]}
+POOL_MIN_SHIFT = {0: 48, 2: 64}
 VECTOR_SHIFTS = {u: [s for s in ALL_SHIFTS if s < first] for u, first in POOL_MIN_SHIFT.items()}
 POOL_SHIFTS = {u: [s for s in ALL_SHIFTS if s >= first] for u, first in POOL_MIN_SHIFT.items()}
 ROW, ORIGIN = 2 * P, P - 1
@@ -81,10 +81,11 @@ def tile_causalwaveletfieldattentionbyte_pa_s_kernel(
         w_rows = const.tile([P, 4, WIDTH], BF16, name="w_rows")
         x0_blocks = x[0].rearrange("(a p) d -> p a d", p=P)
         nc.sync.dma_start(out=x_rows[0][:, 0:2, :], in_=x0_blocks[:, 0:2, :])
-        nc.sync.dma_start(out=small_rows[4 : 4 + SCALES, 0:HEADS], in_=scale_gain)
+        nc.sync.dma_start(out=x_rows[0][:, 2:4, :], in_=x0_blocks[:, 2:4, :])
+        nc.sync.dma_start(out=small_rows[4:12, 0:HEADS], in_=scale_gain[0:8, :])
+        nc.sync.dma_start(out=small_rows[12 : 4 + SCALES, 0:HEADS], in_=scale_gain[8:SCALES, :])
         nc.sync.dma_start(out=small_rows[0:2, :], in_=k_b.rearrange("(a c) -> a c", c=P))
         nc.sync.dma_start(out=small_rows[2:4, :], in_=v_b.rearrange("(a c) -> a c", c=P))
-        nc.sync.dma_start(out=x_rows[0][:, 2:4, :], in_=x0_blocks[:, 2:4, :])
         nc.sync.dma_start(out=w_rows[:, 0:2, :], in_=k_w.rearrange("(a p) d -> p a d", p=P))
         nc.sync.dma_start(out=w_rows[:, 2:4, :], in_=v_w.rearrange("(a p) d -> p a d", p=P))
         nc.sync.dma_start(out=x_rows[1][:], in_=x[1].rearrange("(a p) d -> p a d", p=P))
@@ -220,10 +221,9 @@ def tile_causalwaveletfieldattentionbyte_pa_s_kernel(
             fields[u] = const.tile([P, TOKENS], F32, name="field_%d" % u)
             nc.scalar.activation(out=fields[u][:], in_=field_banks[u][:], func=ACT.Copy, scale=TAPS[3])
 
-        x0_turned = [turned_bank(0, x_rows[0], (0, 1))]
+        x0_turned = [turned_bank(0, x_rows[0], (0, 1)), turned_bank(1, x_rows[0], (2, 3))]
         small_ps = bank(7, [P, P], "small_ps", BF16)
         nc.tensor.transpose(small_ps[:], small_rows[:], ident_bf16[:])
-        x0_turned.append(turned_bank(1, x_rows[0], (2, 3)))
         w0_turned = [turned_bank(2, w_rows, (0,)), turned_bank(3, w_rows, (2,))]
         w1_turned = turned_bank(4, w_rows, (1, 3))
         regroup(nc.vector.tensor_copy, x0_turned[0], x_grouped[0][:, 0 : 2 * P, :])
@@ -254,7 +254,6 @@ def tile_causalwaveletfieldattentionbyte_pa_s_kernel(
 
         quantise_w(CHANNELS, CHANNELS + P)
         project_v(0, 1)
-        x1_turned = [turned_bank(5, x_rows[1], (0, 1))]
         square(0)
         nc.vector.reciprocal(out=total[:], in_=total[:])
         add_v_bias(0)
@@ -292,15 +291,7 @@ def tile_causalwaveletfieldattentionbyte_pa_s_kernel(
         add_squares(0, 2)
         root(0)
         turn_v(0, 3)
-        by_channel_ps = bank(7, [P, HALVES, N_POW2 + N_TRIPLE], "by_channel_ps")
-        for h in range(HALVES):
-            nc.tensor.matmul(
-                out=by_channel_ps[:, h, :],
-                lhsT=spread[:].rearrange("p i c -> p (i c)")[:, h * P : (h + 1) * P],
-                rhs=by_head[:],
-                start=True,
-                stop=True,
-            )
+        x1_turned = [turned_bank(5, x_rows[1], (0, 1))]
         everywhere = bank(2, [P, HEADS_PER_HALF, n_pow2 + n_triple], "everywhere")
         nc.tensor.matmul(
             out=everywhere[:].rearrange("p i t -> p (i t)"),
@@ -323,10 +314,19 @@ def tile_causalwaveletfieldattentionbyte_pa_s_kernel(
                     in_=everywhere[:, :, first + j : first + j + n],
                 )
         x1_turned.append(turned_bank(6, x_rows[1], (2, 3)))
-        regroup(nc.vector.tensor_copy, x1_turned[0], x_grouped[1][:, 0 : 2 * P, :])
         make_field(0)
+        regroup(nc.vector.tensor_copy, x1_turned[0], x_grouped[1][:, 0 : 2 * P, :])
         turn_field(0, 4)
         copy_field(0)
+        by_channel_ps = bank(7, [P, HALVES, N_POW2 + N_TRIPLE], "by_channel_ps")
+        for h in range(HALVES):
+            nc.tensor.matmul(
+                out=by_channel_ps[:, h, :],
+                lhsT=spread[:].rearrange("p i c -> p (i c)")[:, h * P : (h + 1) * P],
+                rhs=by_head[:],
+                start=True,
+                stop=True,
+            )
         regroup(nc.vector.tensor_copy, x1_turned[1], x_grouped[1][:, 2 * P :, :])
         quantise_x(1, 0, 2 * P)
         quantise_w(CHANNELS + P, 2 * CHANNELS)
@@ -346,12 +346,17 @@ def tile_causalwaveletfieldattentionbyte_pa_s_kernel(
             in_=flat[:, 0 : P * (ROW - 1)].rearrange("i (k l) -> k i l", l=ROW - 1)[:, :, ORIGIN : ORIGIN + P],
         )
 
+        def first_row(shift):
+            return -(-shift // CLASSES)
+
         results = [const.tile([P, TOKENS], F32, name="result_%d" % u) for u in range(len(units))]
+        nc.gpsimd.memset(results[3][:, 0 : ODD_SHIFTS[3][0]], 0.0)
         scaled_copies = {}
         for u in (1, 3):
-            nc.gpsimd.memset(results[u][:, 0 : ODD_SHIFTS[0]], 0.0)
-            scaled_copies[u] = const.tile([P, CLASSES, P], F32, name="scaled_copy_%d" % u)
-            nc.gpsimd.memset(scaled_copies[u][:, :, 0:SCALED_FIRST], 0.0)
+            for shift in SCALED_SHIFTS[u]:
+                copy = const.tile([P, CLASSES, P], F32, name="scaled_copy_%d_%d" % (u, shift))
+                nc.gpsimd.memset(copy[:, :, 0 : first_row(shift)], 0.0)
+                scaled_copies[(u, shift)] = copy
         pool_sums, long_banks, long_toks, back_banks = {}, {}, {}, {}
 
         def vector_term(u, r):
@@ -412,15 +417,15 @@ def tile_causalwaveletfieldattentionbyte_pa_s_kernel(
             )
             store(u)
 
-        def scale_copy(u):
-            col = COLUMN[SCALED_SHIFT]
-            rest = SCALED_FIRST * CLASSES - SCALED_SHIFT
+        def scale_copy(u, shift):
+            col, row = COLUMN[shift], first_row(shift)
+            rest = row * CLASSES - shift
             for m, cls, src in (
-                (slice(SCALED_FIRST, P), slice(0, CLASSES), slice(rest, TOKENS - SCALED_SHIFT)),
-                (slice(SCALED_FIRST - 1, SCALED_FIRST), slice(CLASSES - rest, CLASSES), slice(0, rest)),
+                (slice(row, P), slice(0, CLASSES), slice(rest, TOKENS - shift)),
+                (slice(row - 1, row), slice(CLASSES - rest, CLASSES), slice(0, rest)),
             ):
                 nc.scalar.activation(
-                    out=scaled_copies[u][:, cls, m],
+                    out=scaled_copies[(u, shift)][:, cls, m],
                     in_=field_banks[u][:, src].rearrange("p (m r) -> p r m", r=cls.stop - cls.start),
                     func=ACT.Copy,
                     scale=coef[:, 1, col : col + 1],
@@ -437,15 +442,18 @@ def tile_causalwaveletfieldattentionbyte_pa_s_kernel(
                     start=head == 0,
                     stop=False,
                 )
-            for r in range(CLASSES):
-                nc.tensor.matmul(
-                    out=long_banks[u][:, r, :],
-                    lhsT=scaled_copies[u][:, r, :],
-                    rhs=ident_f32[:],
-                    is_transpose=True,
-                    start=False,
-                    stop=r == CLASSES - 1,
-                )
+
+        def add_scaled_copies(u):
+            for shift in SCALED_SHIFTS[u]:
+                for r in range(CLASSES):
+                    nc.tensor.matmul(
+                        out=long_banks[u][:, r, :],
+                        lhsT=scaled_copies[(u, shift)][:, r, :],
+                        rhs=ident_f32[:],
+                        is_transpose=True,
+                        start=False,
+                        stop=shift == SCALED_SHIFTS[u][-1] and r == CLASSES - 1,
+                    )
 
         def copy_long(u):
             long_toks[u] = stage.tile([P, CLASSES, P], F32, name="long_tok")
@@ -457,11 +465,11 @@ def tile_causalwaveletfieldattentionbyte_pa_s_kernel(
                 nc.tensor.transpose(back_banks[u][:, r, :], long_toks[u][:, r, :], ident_f32[:])
 
         def odd_term(u, r):
-            shift = ODD_SHIFTS[r]
+            shift = ODD_SHIFTS[u][r]
             col = COLUMN[shift]
             scale = coef[:, 1, col : col + 1]
             src = field_banks[u][:, 0 : TOKENS - shift]
-            if r == 0:
+            if r == 0 and u == 3:
                 nc.vector.tensor_scalar_mul(out=results[u][:, shift:], in0=src, scalar1=scale)
                 return
             nc.vector.scalar_tensor_tensor(
@@ -471,6 +479,12 @@ def tile_causalwaveletfieldattentionbyte_pa_s_kernel(
                 in1=results[u][:, shift:],
                 op0=ALU.mult,
                 op1=ALU.add,
+            )
+
+        def copy_back(u):
+            nc.scalar.copy(
+                out=results[u][:].rearrange("p (m r) -> p m r", r=CLASSES),
+                in_=back_banks[u][:].rearrange("p r m -> p m r"),
             )
 
         def add_long_and_store(u):
@@ -491,69 +505,74 @@ def tile_causalwaveletfieldattentionbyte_pa_s_kernel(
         turn_v(2, 3)
         pool_term(0, 2)
         vector_term(0, 1)
-        pool_term(0, 3)
         root(2)
         project_k(1, 0)
         project_v(1, 1)
-        pool_term(0, 4)
-        pool_term(0, 5)
+        pool_term(0, 3)
+        square(1)
         vector_term(0, 2)
         vector_term(0, 3)
         vector_term(0, 4)
         vector_term(0, 5)
         make_field(2)
         turn_field(2, 5)
-        square(1)
-        pool_term(0, 6)
-        copy_field(2)
         add_v_bias(1)
         add_squares(1, 2)
         turn_v(1, 3)
-        pool_term(0, 7)
-        vector_term(0, 6)
-        vector_term(0, 7)
-        vector_term(0, 8)
-        pool_term(2, 0)
+        pool_term(0, 4)
+        copy_field(2)
         root(1)
-        pool_term(2, 1)
+        pool_term(0, 5)
         project_k(3, 0)
         project_v(3, 1)
-        vector_term(2, 0)
+        vector_term(0, 6)
+        vector_term(0, 7)
+        square(3)
+        vector_term(0, 8)
         make_field(1)
         turn_field(1, 6)
-        square(3)
-        vector_term(2, 1)
-        pool_term(2, 2)
-        vector_term(2, 2)
+        vector_term(0, 9)
         add_v_bias(3)
         add_squares(3, 2)
         turn_v(3, 3)
-        scale_copy(1)
+        pool_term(0, 6)
+        pool_term(2, 0)
         root(3)
+        pool_term(2, 1)
+        for shift in SCALED_SHIFTS[1]:
+            scale_copy(1, shift)
+        vector_term(2, 0)
+        vector_term(2, 1)
+        vector_term(2, 2)
         filter_classes(1, 0)
-        join_on_gpsimd_and_store(0)
-        pool_term(2, 3)
-        vector_term(2, 3)
-        pool_term(2, 4)
-        vector_term(2, 4)
+        add_scaled_copies(1)
         make_field(3)
         turn_field(3, 7)
-        vector_term(2, 5)
+        join_on_gpsimd_and_store(0)
+        vector_term(2, 3)
+        pool_term(2, 2)
+        pool_term(2, 3)
         copy_long(1)
-        turn_long(1, 2)
-        scale_copy(3)
+        for shift in SCALED_SHIFTS[3]:
+            scale_copy(3, shift)
         filter_classes(3, 1)
-        pool_term(2, 5)
-        pool_term(2, 6)
+        turn_long(1, 2)
+        add_scaled_copies(3)
+        vector_term(2, 4)
+        vector_term(2, 5)
+        copy_back(1)
+        pool_term(2, 4)
         vector_term(2, 6)
+        pool_term(2, 5)
         vector_term(2, 7)
         vector_term(2, 8)
-        vector_term(2, 9)
         copy_long(3)
         turn_long(3, 3)
-        for r in range(len(ODD_SHIFTS)):
-            odd_term(1, r)
-            odd_term(3, r)
-        add_long_and_store(1)
-        join_and_store(2)
+        vector_term(2, 9)
+        vector_term(2, 10)
+        odd_term(3, 0)
+        odd_term(1, 0)
+        odd_term(3, 1)
+        store(1)
         add_long_and_store(3)
+        join_and_store(2)

from contextlib import ExitStack

import concourse.mybir as mybir
from concourse.masks import make_identity

F32 = mybir.dt.float32
BF16 = mybir.dt.bfloat16
U32 = mybir.dt.uint32
U8 = mybir.dt.uint8
FP8X4 = mybir.dt.float8_e4m3fn_x4
ALU = mybir.AluOpType
ACT = mybir.ActivationFunctionType
AXIS = mybir.AxisListType

P = 128
BATCH, TOKENS, WIDTH, CHANNELS, HEADS, SCALES = 2, 512, 512, 256, 16, 10
HEAD_DIM = CHANNELS // HEADS
HALVES = CHANNELS // P
HEADS_PER_HALF = P // HEAD_DIM
TOKEN_BLOCKS = TOKENS // P
TAPS = (0.4829629131445341, 0.8365163037378079, 0.2241438680420134, -0.1294095225512604)

CLASSES = 4

FLOPS = 2 * BATCH * TOKENS * WIDTH * 2 * CHANNELS

POW2_SHIFTS = [2**i for i in range(SCALES) if 2**i < TOKENS]
TRIPLE_SHIFTS = [3 * 2**j for j in range(SCALES) if 3 * 2**j < TOKENS]
N_POW2, N_TRIPLE = len(POW2_SHIFTS), len(TRIPLE_SHIFTS)
COLUMN = {s: i for i, s in enumerate(POW2_SHIFTS + TRIPLE_SHIFTS)}
ALL_SHIFTS = sorted(COLUMN)
CLASS_CHANGES = [s for s in ALL_SHIFTS if s % CLASSES]
ODD_SHIFTS = {1: CLASS_CHANGES[:1], 3: CLASS_CHANGES[:2]}
SCALED_SHIFTS = {1: CLASS_CHANGES[1:], 3: CLASS_CHANGES[2:]}
POOL_MIN_SHIFT = {0: 48, 2: 64}
VECTOR_SHIFTS = {u: [s for s in ALL_SHIFTS if s < first] for u, first in POOL_MIN_SHIFT.items()}
POOL_SHIFTS = {u: [s for s in ALL_SHIFTS if s >= first] for u, first in POOL_MIN_SHIFT.items()}
ROW, ORIGIN = 2 * P, P - 1


def turn(nc, turned, rows_bf16, blocks, ident_f32):
    words = rows_bf16.bitcast(F32)
    for i, a in enumerate(blocks):
        for u in range(2):
            nc.tensor.transpose(turned[:, u, i * P : (i + 1) * P], words[:, a, u : 2 * P : 2], ident_f32)


def regroup(copy, turned, grouped):
    copy(out=grouped.bitcast(F32), in_=turned.rearrange("p u c -> p c u"))


def quantise(nc, grouped, codes, scales):
    nc.vector.quantize_mx(
        out=codes.bitcast(FP8X4), scales=scales, in_=grouped.rearrange("p c t -> p (c t)")
    )


def tile_causalwaveletfieldattentionbyte_pa_s_kernel(
    tc, x, k_w, k_b, v_w, v_b, scale_gain, out
):
    nc = tc.nc
    with ExitStack() as stack:
        const = stack.enter_context(tc.tile_pool(name="const", bufs=1))
        stage = stack.enter_context(tc.tile_pool(name="stage", bufs=2))
        planes = stack.enter_context(tc.tile_pool(name="planes", bufs=8))
        banks = stack.enter_context(tc.psum_pool(name="banks", bufs=1))
        stack.enter_context(tc.manual_schedule())

        def bank(i, shape, name, dtype=F32):
            return banks.tile(shape, dtype, name=name, tag="bank_%d" % i)

        small_rows = const.tile([P, P], BF16, name="small_rows")
        nc.gpsimd.memset(small_rows[:], 0.0)
        table_warm = const.tile([P, 1], F32, name="table_warm")
        nc.vector.memset(table_warm[:], 1.0)
        nc.scalar.activation(out=table_warm[:], in_=table_warm[:], func=ACT.Exp)

        x_rows = [
            const.tile([P, TOKEN_BLOCKS, WIDTH], BF16, name="x_rows_%d" % b) for b in range(BATCH)
        ]
        w_rows = const.tile([P, 4, WIDTH], BF16, name="w_rows")
        x0_blocks = x[0].rearrange("(a p) d -> p a d", p=P)
        nc.sync.dma_start(out=x_rows[0][:, 0:2, :], in_=x0_blocks[:, 0:2, :])
        nc.sync.dma_start(out=x_rows[0][:, 2:4, :], in_=x0_blocks[:, 2:4, :])
        nc.sync.dma_start(out=small_rows[4:12, 0:HEADS], in_=scale_gain[0:8, :])
        nc.sync.dma_start(out=small_rows[12 : 4 + SCALES, 0:HEADS], in_=scale_gain[8:SCALES, :])
        nc.sync.dma_start(out=small_rows[0:2, :], in_=k_b.rearrange("(a c) -> a c", c=P))
        nc.sync.dma_start(out=small_rows[2:4, :], in_=v_b.rearrange("(a c) -> a c", c=P))
        nc.sync.dma_start(out=w_rows[:, 0:2, :], in_=k_w.rearrange("(a p) d -> p a d", p=P))
        nc.sync.dma_start(out=w_rows[:, 2:4, :], in_=v_w.rearrange("(a p) d -> p a d", p=P))
        nc.sync.dma_start(out=x_rows[1][:], in_=x[1].rearrange("(a p) d -> p a d", p=P))

        ident_f32 = const.tile([P, P], F32, name="ident_f32")
        make_identity(nc, ident_f32[:])
        ident_bf16 = const.tile([P, P], BF16, name="ident_bf16")
        nc.vector.tensor_copy(out=ident_bf16[:], in_=ident_f32[:])
        ones = const.tile([P, P], F32, name="ones")
        nc.vector.memset(ones[:], 1.0)
        head_of = const.tile([P, HEADS_PER_HALF], F32, name="head_of")
        nc.vector.tensor_reduce(
            out=head_of[:],
            in_=ident_f32[:].rearrange("p (i c) -> p i c", c=HEAD_DIM),
            axis=AXIS.X,
            op=ALU.add,
        )
        spread = const.tile([P, HEADS, HEAD_DIM], F32, name="spread")
        nc.vector.tensor_copy(
            out=spread[:], in_=ident_f32[:, 0:HEADS].unsqueeze(2).to_broadcast([P, HEADS, HEAD_DIM])
        )
        filter_rows = const.tile([P, HEADS_PER_HALF, ROW], F32, name="filter_rows")
        nc.gpsimd.memset(filter_rows[:], 0.0)

        x_grouped = [
            const.tile([P, TOKENS, 4], BF16, name="x_grouped_%d" % b, align_bytes=64) for b in range(BATCH)
        ]
        x_codes = [const.tile([P, TOKENS], U32, name="x_codes_%d" % b, align_bytes=64) for b in range(BATCH)]
        x_scales = [const.tile([P, TOKENS], U8, name="x_scales_%d" % b, align_bytes=64) for b in range(BATCH)]
        w_grouped = const.tile([P, 2 * CHANNELS, 4], BF16, name="w_grouped", align_bytes=64)
        w_codes = const.tile([P, 2 * CHANNELS], U32, name="w_codes", align_bytes=64)
        w_scales = const.tile([P, 2 * CHANNELS], U8, name="w_scales", align_bytes=64)

        def turned_bank(i, rows, blocks):
            turned = bank(i, [P, 2, len(blocks) * P], "turned")
            turn(nc, turned[:], rows[:], blocks, ident_f32[:])
            return turned[:]

        def quantise_x(b, first, last):
            cols = slice(first, last)
            quantise(nc, x_grouped[b][:, cols, :], x_codes[b][:, cols], x_scales[b][:, cols])

        def quantise_w(first, last):
            cols = slice(first, last)
            quantise(nc, w_grouped[:, cols, :], w_codes[:, cols], w_scales[:, cols])

        units = [(b, h) for b in range(BATCH) for h in range(HALVES)]
        k_banks, v_banks, squares, v_full, norm_banks, norms = {}, {}, {}, {}, {}, {}
        v_toks, f_toks, field_banks, fields = {}, {}, {}, {}

        def project(u, which, i):
            b, h = units[u]
            cols = slice(which * CHANNELS + h * P, which * CHANNELS + (h + 1) * P)
            proj = bank(i, [P, TOKENS], "proj")
            nc.tensor.matmul_mx(
                out=proj[:],
                lhsT=w_codes[:, cols].bitcast(FP8X4),
                lhsT_scale=w_scales[:, cols],
                rhs=x_codes[b][:].bitcast(FP8X4),
                rhs_scale=x_scales[b][:],
                start=True,
                stop=True,
            )
            return proj

        def project_k(u, i):
            k_banks[u] = project(u, 0, i)

        def project_v(u, i):
            v_banks[u] = project(u, 1, i)

        def by_block(u, tile):
            if units[u][1] == 0:
                return tile.rearrange("p (a m) -> p a m", m=P)
            return tile.rearrange("p (m r) -> p r m", r=CLASSES)

        def square(u):
            h = units[u][1]
            squares[u] = stage.tile([P, TOKEN_BLOCKS, P], F32, name="k_square")
            nc.scalar.activation(
                out=squares[u][:],
                in_=by_block(u, k_banks[u][:]),
                func=ACT.Square,
                bias=bias[:, 0, h : h + 1],
                scale=1.0,
            )

        def add_v_bias(u):
            h = units[u][1]
            v_full[u] = stage.tile([P, TOKEN_BLOCKS, P], F32, name="v_full")
            nc.scalar.activation(
                out=v_full[u][:],
                in_=by_block(u, v_banks[u][:]),
                func=ACT.Identity,
                bias=bias[:, 1, h : h + 1],
                scale=1.0,
            )

        def add_squares(u, i):
            norm_banks[u] = bank(i, [P, TOKEN_BLOCKS, HEADS_PER_HALF], "norm_ps")
            for a in range(TOKEN_BLOCKS):
                nc.tensor.matmul(
                    out=norm_banks[u][:, a, :], lhsT=squares[u][:, a, :], rhs=head_of[:], start=True, stop=True
                )

        def root(u):
            norms[u] = stage.tile([P, TOKEN_BLOCKS, HEADS_PER_HALF], F32, name="norm")
            nc.scalar.activation(out=norms[u][:], in_=norm_banks[u][:], func=ACT.Sqrt)

        def turn_v(u, i):
            v_toks[u] = bank(i, [P, TOKEN_BLOCKS, P], "v_tok")
            for a in range(TOKEN_BLOCKS):
                nc.tensor.transpose(v_toks[u][:, a, :], v_full[u][:, a, :], ident_f32[:])

        def make_field(u):
            f_toks[u] = const.tile([P, TOKEN_BLOCKS, P], F32, name="f_tok_%d" % u)
            nc.vector.tensor_tensor(
                out=f_toks[u][:].rearrange("p a (i c) -> p (a i) c", c=HEAD_DIM),
                in0=v_toks[u][:].rearrange("p a (i c) -> p (a i) c", c=HEAD_DIM),
                in1=norms[u][:]
                .rearrange("p a i -> p (a i)")
                .unsqueeze(2)
                .to_broadcast([P, TOKEN_BLOCKS * HEADS_PER_HALF, HEAD_DIM]),
                op=ALU.mult,
            )

        def turn_field(u, i):
            field_banks[u] = bank(i, [P, TOKENS], "field_ps")
            for a in range(TOKEN_BLOCKS):
                nc.tensor.transpose(by_block(u, field_banks[u][:])[:, a, :], f_toks[u][:, a, :], ident_f32[:])

        def copy_field(u):
            fields[u] = const.tile([P, TOKENS], F32, name="field_%d" % u)
            nc.scalar.activation(out=fields[u][:], in_=field_banks[u][:], func=ACT.Copy, scale=TAPS[3])

        x0_turned = [turned_bank(0, x_rows[0], (0, 1)), turned_bank(1, x_rows[0], (2, 3))]
        small_ps = bank(7, [P, P], "small_ps", BF16)
        nc.tensor.transpose(small_ps[:], small_rows[:], ident_bf16[:])
        w0_turned = [turned_bank(2, w_rows, (0,)), turned_bank(3, w_rows, (2,))]
        w1_turned = turned_bank(4, w_rows, (1, 3))
        regroup(nc.vector.tensor_copy, x0_turned[0], x_grouped[0][:, 0 : 2 * P, :])
        regroup(nc.scalar.copy, x0_turned[1], x_grouped[0][:, 2 * P :, :])

        logits = small_ps[:, 4 : 4 + SCALES]
        minus_top = const.tile([P, 1], F32, name="minus_top")
        nc.vector.tensor_reduce(out=minus_top[:], in_=logits, axis=AXIS.X, op=ALU.max, negate=True)
        bias = const.tile([P, 2, HALVES], F32, name="bias")
        nc.vector.tensor_copy(out=bias[:].rearrange("p w h -> p (w h)"), in_=small_ps[:, 0 : 2 * HALVES])
        gain = const.tile([P, SCALES], F32, name="gain")
        total = const.tile([P, 1], F32, name="total")
        nc.scalar.activation(
            out=gain[:], in_=logits, func=ACT.Exp, bias=minus_top[:, 0:1], scale=1.0, accum_out=total[:]
        )
        nc.scalar.activation(out=table_warm[:], in_=ones[:, 0:1], func=ACT.Sqrt)

        def regroup_w(copy, turned, which):
            first = which * CHANNELS
            regroup(copy, turned, w_grouped[:, first : first + P, :])

        quantise_x(0, 0, 2 * P)
        regroup_w(nc.vector.tensor_copy, w0_turned[0], 0)
        quantise_x(0, 2 * P, TOKENS)
        quantise_w(0, P)
        project_k(0, 0)
        regroup_w(nc.vector.tensor_copy, w0_turned[1], 1)

        quantise_w(CHANNELS, CHANNELS + P)
        project_v(0, 1)
        square(0)
        nc.vector.reciprocal(out=total[:], in_=total[:])
        add_v_bias(0)
        nc.vector.tensor_scalar_mul(out=gain[:], in0=gain[:], scalar1=total[:, 0:1])
        nc.vector.tensor_copy(
            out=w_grouped[:].bitcast(F32).rearrange("p (w h c) u -> p w h c u", w=2, h=HALVES)[:, :, 1, :, :],
            in_=w1_turned.rearrange("p u (w c) -> p w c u", w=2),
        )
        by_head = const.tile([P, N_POW2 + N_TRIPLE], F32, name="by_head")
        nc.vector.tensor_scalar_mul(out=by_head[:, 0:N_POW2], in0=gain[:, 0:N_POW2], scalar1=TAPS[2])
        nc.vector.tensor_scalar_mul(out=by_head[:, N_POW2:], in0=gain[:, 0:N_TRIPLE], scalar1=TAPS[0])
        quantise_w(P, CHANNELS)
        nc.vector.scalar_tensor_tensor(
            out=by_head[:, 1:N_POW2],
            in0=gain[:, 0 : N_POW2 - 1],
            scalar=TAPS[1],
            in1=by_head[:, 1:N_POW2],
            op0=ALU.mult,
            op1=ALU.add,
        )
        first_pow2, first_triple = POW2_SHIFTS.index(CLASSES), TRIPLE_SHIFTS.index(3 * CLASSES)
        n_pow2, n_triple = N_POW2 - first_pow2, N_TRIPLE - first_triple
        apart = const.tile([P, HEADS_PER_HALF, n_pow2 + n_triple], F32, name="apart")
        for dest, first, count in (
            (apart[:, :, 0:n_pow2], first_pow2, n_pow2),
            (apart[:, :, n_pow2:], N_POW2 + first_triple, n_triple),
        ):
            shape = [P, HEADS_PER_HALF, count]
            nc.gpsimd.tensor_tensor(
                out=dest,
                in0=ident_f32[:, HEADS_PER_HALF:HEADS].unsqueeze(2).to_broadcast(shape),
                in1=by_head[:, first : first + count].unsqueeze(1).to_broadcast(shape),
                op=ALU.mult,
            )
        add_squares(0, 2)
        root(0)
        turn_v(0, 3)
        x1_turned = [turned_bank(5, x_rows[1], (0, 1))]
        everywhere = bank(2, [P, HEADS_PER_HALF, n_pow2 + n_triple], "everywhere")
        nc.tensor.matmul(
            out=everywhere[:].rearrange("p i t -> p (i t)"),
            lhsT=ones[:],
            rhs=apart[:].rearrange("p i t -> p (i t)"),
            start=True,
            stop=True,
        )
        nc.scalar.activation(
            out=filter_rows[:, :, ORIGIN : ORIGIN + 1],
            in_=ones[:, 0:HEADS_PER_HALF].unsqueeze(2),
            func=ACT.Copy,
            scale=TAPS[3],
        )
        for first, count, factor in ((0, n_pow2, 1), (n_pow2, n_triple, 3)):
            for j in range(0, count, 2):
                i, n = factor * 2**j, min(2, count - j)
                nc.scalar.copy(
                    out=filter_rows[:, :, ORIGIN + i : ORIGIN + i + (n - 1) * i + 1 : i],
                    in_=everywhere[:, :, first + j : first + j + n],
                )
        x1_turned.append(turned_bank(6, x_rows[1], (2, 3)))
        make_field(0)
        regroup(nc.vector.tensor_copy, x1_turned[0], x_grouped[1][:, 0 : 2 * P, :])
        turn_field(0, 4)
        copy_field(0)
        by_channel_ps = bank(7, [P, HALVES, N_POW2 + N_TRIPLE], "by_channel_ps")
        for h in range(HALVES):
            nc.tensor.matmul(
                out=by_channel_ps[:, h, :],
                lhsT=spread[:].rearrange("p i c -> p (i c)")[:, h * P : (h + 1) * P],
                rhs=by_head[:],
                start=True,
                stop=True,
            )
        regroup(nc.vector.tensor_copy, x1_turned[1], x_grouped[1][:, 2 * P :, :])
        quantise_x(1, 0, 2 * P)
        quantise_w(CHANNELS + P, 2 * CHANNELS)
        coef = const.tile([P, HALVES, N_POW2 + N_TRIPLE], F32, name="coef")
        nc.vector.tensor_copy(out=coef[:], in_=by_channel_ps[:])
        coef_over_tap3 = const.tile([P, N_POW2 + N_TRIPLE], F32, name="coef_over_tap3")
        nc.vector.tensor_scalar_mul(out=coef_over_tap3[:], in0=by_channel_ps[:, 0, :], scalar1=1.0 / TAPS[3])
        quantise_x(1, 2 * P, TOKENS)
        project_k(2, 0)
        project_v(2, 1)

        flat = out.rearrange("b c n -> (b c n)").rearrange("(i k) -> i k", k=P * ROW)
        nc.sync.dma_start(out=flat.rearrange("i (k l) -> k i l", l=ROW), in_=filter_rows[:])
        toeplitz = const.tile([P, HEADS_PER_HALF, P], F32, name="toeplitz")
        nc.sync.dma_start(
            out=toeplitz[:],
            in_=flat[:, 0 : P * (ROW - 1)].rearrange("i (k l) -> k i l", l=ROW - 1)[:, :, ORIGIN : ORIGIN + P],
        )

        def first_row(shift):
            return -(-shift // CLASSES)

        results = [const.tile([P, TOKENS], F32, name="result_%d" % u) for u in range(len(units))]
        nc.gpsimd.memset(results[3][:, 0 : ODD_SHIFTS[3][0]], 0.0)
        scaled_copies = {}
        for u in (1, 3):
            for shift in SCALED_SHIFTS[u]:
                copy = const.tile([P, CLASSES, P], F32, name="scaled_copy_%d_%d" % (u, shift))
                nc.gpsimd.memset(copy[:, :, 0 : first_row(shift)], 0.0)
                scaled_copies[(u, shift)] = copy
        pool_sums, long_banks, long_toks, back_banks = {}, {}, {}, {}

        def vector_term(u, r):
            shift = VECTOR_SHIFTS[u][r]
            col = COLUMN[shift]
            base = fields[u]
            if r == 0:
                nc.vector.tensor_copy(out=results[u][:, 0:shift], in_=base[:, 0:shift])
            for first, last in ((shift, TOKENS // 2), (TOKENS // 2, TOKENS)):
                nc.vector.scalar_tensor_tensor(
                    out=results[u][:, first:last],
                    in0=field_banks[u][:, first - shift : last - shift],
                    scalar=coef[:, 0, col : col + 1],
                    in1=(base if r == 0 else results[u])[:, first:last],
                    op0=ALU.mult,
                    op1=ALU.add,
                )

        def pool_term(u, r):
            shift = POOL_SHIFTS[u][r]
            col = COLUMN[shift]
            if r == 0:
                pool_sums[u] = stage.tile([P, TOKENS], F32, name="pool_sum")
            scaled = pool_sums[u] if r == 0 else planes.tile([P, TOKENS], F32, name="plane")
            nc.scalar.activation(
                out=scaled[:, shift:],
                in_=fields[u][:, 0 : TOKENS - shift],
                func=ACT.Copy,
                scale=coef_over_tap3[:, col : col + 1],
            )
            if r > 0:
                nc.gpsimd.tensor_tensor(
                    out=pool_sums[u][:, shift:], in0=pool_sums[u][:, shift:], in1=scaled[:, shift:], op=ALU.add
                )

        def store(u, part=None):
            b, h = units[u]
            cols = slice(0, TOKENS) if part is None else slice(part * TOKENS // 2, (part + 1) * TOKENS // 2)
            nc.sync.dma_start(out=out[b, h * P : (h + 1) * P, cols], in_=results[u][:, cols])

        def join_and_store(u):
            first_shift = POOL_SHIFTS[u][0]
            nc.vector.tensor_tensor(
                out=results[u][:, first_shift:],
                in0=results[u][:, first_shift:],
                in1=pool_sums[u][:, first_shift:],
                op=ALU.add,
            )
            store(u)

        def join_on_gpsimd_and_store(u):
            first_shift = POOL_SHIFTS[u][0]
            nc.gpsimd.tensor_tensor(
                out=results[u][:, first_shift:],
                in0=results[u][:, first_shift:],
                in1=pool_sums[u][:, first_shift:],
                op=ALU.add,
            )
            store(u)

        def scale_copy(u, shift):
            col, row = COLUMN[shift], first_row(shift)
            rest = row * CLASSES - shift
            for m, cls, src in (
                (slice(row, P), slice(0, CLASSES), slice(rest, TOKENS - shift)),
                (slice(row - 1, row), slice(CLASSES - rest, CLASSES), slice(0, rest)),
            ):
                nc.scalar.activation(
                    out=scaled_copies[(u, shift)][:, cls, m],
                    in_=field_banks[u][:, src].rearrange("p (m r) -> p r m", r=cls.stop - cls.start),
                    func=ACT.Copy,
                    scale=coef[:, 1, col : col + 1],
                )

        def filter_classes(u, i):
            long_banks[u] = bank(i, [P, CLASSES, P], "long_ps")
            for head in range(HEADS_PER_HALF):
                cols = slice(head * HEAD_DIM, (head + 1) * HEAD_DIM)
                nc.tensor.matmul(
                    out=long_banks[u][:, :, cols],
                    lhsT=toeplitz[:, head, :],
                    rhs=f_toks[u][:, :, cols],
                    start=head == 0,
                    stop=False,
                )

        def add_scaled_copies(u):
            for shift in SCALED_SHIFTS[u]:
                for r in range(CLASSES):
                    nc.tensor.matmul(
                        out=long_banks[u][:, r, :],
                        lhsT=scaled_copies[(u, shift)][:, r, :],
                        rhs=ident_f32[:],
                        is_transpose=True,
                        start=False,
                        stop=shift == SCALED_SHIFTS[u][-1] and r == CLASSES - 1,
                    )

        def copy_long(u):
            long_toks[u] = stage.tile([P, CLASSES, P], F32, name="long_tok")
            nc.scalar.copy(out=long_toks[u][:], in_=long_banks[u][:])

        def turn_long(u, i):
            back_banks[u] = bank(i, [P, CLASSES, P], "back_ps")
            for r in range(CLASSES):
                nc.tensor.transpose(back_banks[u][:, r, :], long_toks[u][:, r, :], ident_f32[:])

        def odd_term(u, r):
            shift = ODD_SHIFTS[u][r]
            col = COLUMN[shift]
            scale = coef[:, 1, col : col + 1]
            src = field_banks[u][:, 0 : TOKENS - shift]
            if r == 0 and u == 3:
                nc.vector.tensor_scalar_mul(out=results[u][:, shift:], in0=src, scalar1=scale)
                return
            nc.vector.scalar_tensor_tensor(
                out=results[u][:, shift:],
                in0=src,
                scalar=scale,
                in1=results[u][:, shift:],
                op0=ALU.mult,
                op1=ALU.add,
            )

        def copy_back(u):
            nc.scalar.copy(
                out=results[u][:].rearrange("p (m r) -> p m r", r=CLASSES),
                in_=back_banks[u][:].rearrange("p r m -> p m r"),
            )

        def add_long_and_store(u):
            nc.vector.tensor_tensor(
                out=results[u][:].rearrange("p (m r) -> p m r", r=CLASSES),
                in0=results[u][:].rearrange("p (m r) -> p m r", r=CLASSES),
                in1=back_banks[u][:].rearrange("p r m -> p m r"),
                op=ALU.add,
            )
            store(u)

        pool_term(0, 0)
        pool_term(0, 1)
        square(2)
        vector_term(0, 0)
        add_v_bias(2)
        add_squares(2, 2)
        turn_v(2, 3)
        pool_term(0, 2)
        vector_term(0, 1)
        root(2)
        project_k(1, 0)
        project_v(1, 1)
        pool_term(0, 3)
        square(1)
        vector_term(0, 2)
        vector_term(0, 3)
        vector_term(0, 4)
        vector_term(0, 5)
        make_field(2)
        turn_field(2, 5)
        add_v_bias(1)
        add_squares(1, 2)
        turn_v(1, 3)
        pool_term(0, 4)
        copy_field(2)
        root(1)
        pool_term(0, 5)
        project_k(3, 0)
        project_v(3, 1)
        vector_term(0, 6)
        vector_term(0, 7)
        square(3)
        vector_term(0, 8)
        make_field(1)
        turn_field(1, 6)
        vector_term(0, 9)
        add_v_bias(3)
        add_squares(3, 2)
        turn_v(3, 3)
        pool_term(0, 6)
        pool_term(2, 0)
        root(3)
        pool_term(2, 1)
        for shift in SCALED_SHIFTS[1]:
            scale_copy(1, shift)
        vector_term(2, 0)
        vector_term(2, 1)
        vector_term(2, 2)
        filter_classes(1, 0)
        add_scaled_copies(1)
        make_field(3)
        turn_field(3, 7)
        join_on_gpsimd_and_store(0)
        vector_term(2, 3)
        pool_term(2, 2)
        pool_term(2, 3)
        copy_long(1)
        for shift in SCALED_SHIFTS[3]:
            scale_copy(3, shift)
        filter_classes(3, 1)
        turn_long(1, 2)
        add_scaled_copies(3)
        vector_term(2, 4)
        vector_term(2, 5)
        copy_back(1)
        pool_term(2, 4)
        vector_term(2, 6)
        pool_term(2, 5)
        vector_term(2, 7)
        vector_term(2, 8)
        copy_long(3)
        turn_long(3, 3)
        vector_term(2, 9)
        vector_term(2, 10)
        odd_term(3, 0)
        odd_term(1, 0)
        odd_term(3, 1)
        store(1)
        add_long_and_store(3)
        join_and_store(2)
